import numpy as np
import ml_dtypes


def mxq(x, axis, fmt="e4m3"):
    dtype, down = {"e4m3": (ml_dtypes.float8_e4m3fn, 7), "e5m2": (ml_dtypes.float8_e5m2, 14)}[fmt]
    v = np.moveaxis(np.asarray(x, np.float32).astype(ml_dtypes.bfloat16).astype(np.float64), axis, -1)
    blocks = v.reshape(v.shape[:-1] + (-1, 32))
    amax = np.abs(blocks).max(-1, keepdims=True)
    byte = np.maximum(np.where(amax > 0, np.frexp(amax)[1] - 1 + 127, 0) - down, 1)
    scale = np.exp2(byte - 127.0)
    codes = (blocks / scale).astype(np.float32).astype(dtype).astype(np.float64)
    return np.moveaxis((codes * scale).reshape(v.shape), -1, axis)


WIDE = False


def mx_kscale(k):
    if not WIDE:
        return np.ones(k)
    levels = np.array([10, -10, 5, -5, 0])
    a = np.random.permutation(np.resize(levels, k // 512 * 4)).reshape(k // 512, 4)
    idx = np.arange(k)
    return np.exp2(a[idx // 512, idx % 128 // 32])


BF16 = ml_dtypes.bfloat16


def bf(x):
    return np.asarray(x, np.float32).astype(BF16)


def f64(x):
    return np.asarray(x).astype(np.float64)


E2M1 = np.array([0.0, 0.5, 1.0, 1.5, 2.0, 3.0, 4.0, 6.0, -0.0, -0.5, -1.0, -1.5, -2.0, -3.0, -4.0, -6.0])


def pack_weight(w, fmt):
    k, n = w.shape
    w = f64(bf(w)).reshape(k // 32, 32, n)
    amax = np.abs(w).max(1)
    if fmt == "e4m3":
        byte = np.frexp(amax)[1] - 1 + 127 - 7
    else:
        mant, ex = np.frexp(amax / 6.0)
        byte = np.where(mant > 0.5, ex, ex - 1) + 127
    byte = np.clip(np.where(amax > 0, byte, 1), 1, 254)
    scaled = (w * np.exp2(127.0 - byte)[:, None, :]).reshape(k, n).astype(np.float32)
    by_word = np.ascontiguousarray(scaled.reshape(k // 512, 128, 4, n).transpose(0, 1, 3, 2))
    if fmt == "e4m3":
        words = by_word.astype(ml_dtypes.float8_e4m3fn).view(np.uint8)
    else:
        c = by_word.astype(ml_dtypes.float4_e2m1fn).view(np.uint8) & 0xF
        words = c[..., 0::2] | (c[..., 1::2] << 4)
    return np.ascontiguousarray(words), np.ascontiguousarray(byte.astype(np.uint8).reshape(k // 512, 16, n))


def unpack_weight(words, scales, fmt):
    g, p, n, _ = words.shape
    if fmt == "e4m3":
        vals = np.ascontiguousarray(words).view(ml_dtypes.float8_e4m3fn).astype(np.float64)
    else:
        nib = np.empty((g, p, n, 4), np.uint8)
        nib[..., 0::2] = words & 0xF
        nib[..., 1::2] = words >> 4
        vals = E2M1[nib]
    vals = vals * np.repeat(np.exp2(scales.astype(np.float64) - 127.0), 8, axis=1)[..., None]
    return vals.transpose(0, 1, 3, 2).reshape(g * 512, n)


B, S, D, H, DN, DR, DV, RQ, RKV = 4, 1024, 512, 8, 64, 64, 128, 512, 512
THETA = 10000.0
EPS = 1e-6
FMT = "e4m3"


def rmsnorm(v, w):
    return v * (1.0 / np.sqrt(np.mean(v * v, axis=-1, keepdims=True) + EPS)) * w


def rotate_half(v):
    v1 = v[..., ::2]
    v2 = v[..., 1::2]
    return np.stack((-v2, v1), axis=-1).reshape(v.shape)


def rope_cache():
    inv_freq = 1.0 / THETA ** (np.arange(0, DR, 2) / DR)
    freqs = np.outer(np.arange(S), inv_freq)
    emb = np.concatenate((freqs, freqs), -1)
    return np.cos(emb), np.sin(emb)


def apply_rope(v, cos, sin):
    return v * cos[None, None] + rotate_half(v) * sin[None, None]


def setup_inputs():
    s, t = mx_kscale(D), mx_kscale(RQ)
    x = bf(np.random.standard_normal((B, S, D)) * s)
    Wqa_words, Wqa_scales = pack_weight(np.random.standard_normal((D, RQ)) / np.sqrt(D) / s[:, None], FMT)
    q_a_norm_w = bf((1.0 + 0.1 * np.random.standard_normal(RQ)) * t)
    Wqb_words, Wqb_scales = pack_weight(np.random.standard_normal((RQ, H * (DN + DR))) / np.sqrt(RQ) / t[:, None], FMT)
    return {"x": x,
            "Wqa_words": Wqa_words,
            "Wqa_scales": Wqa_scales,
            "q_a_norm_w": q_a_norm_w,
            "Wqb_words": Wqb_words,
            "Wqb_scales": Wqb_scales}


def reference(x, Wqa_words, Wqa_scales, q_a_norm_w, Wqb_words, Wqb_scales):
    c = mxq(f64(x), 2, "e4m3") @ unpack_weight(Wqa_words, Wqa_scales, FMT)
    h = rmsnorm(c, f64(q_a_norm_w))
    q = mxq(h, 2, "e4m3") @ unpack_weight(Wqb_words, Wqb_scales, FMT)
    q = q.reshape(B, S, H, DN + DR).transpose(0, 2, 1, 3)
    q_nope, q_rope = q[..., :DN], q[..., DN:]
    cos, sin = rope_cache()
    q_rope = apply_rope(q_rope, cos, sin)
    return np.concatenate([q_nope, q_rope], -1)

@@ -1,0 +1,285 @@
+import math
+from contextlib import ExitStack
+
+import concourse.masks as masks
+import concourse.mybir as mybir
+
+F32 = mybir.dt.float32
+BF16 = mybir.dt.bfloat16
+I32 = mybir.dt.int32
+U32 = mybir.dt.uint32
+U8 = mybir.dt.uint8
+FP8X4 = mybir.dt.float8_e4m3fn_x4
+ALU = mybir.AluOpType
+ACT = mybir.ActivationFunctionType
+
+P = 128
+BATCH, SEQ, D_MODEL = 4, 1024, 512
+HEADS, D_NOPE, D_ROPE = 8, 64, 64
+RANK = 512
+HALF_COLS = HEADS * D_NOPE
+THETA = 10000.0
+EPS = 1e-6
+
+POS_PER_PART = SEQ // P
+TILES = 2
+GROUPS_PER_BATCH = POS_PER_PART // TILES
+N_GROUPS = BATCH * GROUPS_PER_BATCH
+WORDS = D_MODEL // 2
+
+N_ANGLES = D_ROPE // 2
+PAIRS = N_ANGLES // 2
+ROUND_MAGIC = 1.5 * 2.0**23
+
+FLOPS = 2 * BATCH * SEQ * (D_MODEL * RANK + RANK * 2 * HALF_COLS)
+
+
+def tile_multiheadlatentattention_pa_t_kernel(
+    tc, x, Wqa_words, Wqa_scales, q_a_norm_w, Wqb_words, Wqb_scales, out
+):
+    nc = tc.nc
+    x_view = x.rearrange("b (p t) k -> b p t k", t=POS_PER_PART)
+    out_view = out.rearrange("b h (p t) d -> b p h t d", t=POS_PER_PART)
+
+    with ExitStack() as ctx:
+        consts = ctx.enter_context(tc.tile_pool(name="consts", bufs=1))
+        work = ctx.enter_context(tc.tile_pool(name="work", bufs=2))
+        outs = ctx.enter_context(tc.tile_pool(name="outs", bufs=3))
+        psum_t = ctx.enter_context(tc.psum_pool(name="psum_t", bufs=1))
+        psum_mm = ctx.enter_context(tc.psum_pool(name="psum_mm", bufs=TILES))
+        ctx.enter_context(tc.manual_schedule())
+
+        wqa_scales = consts.tile([P, RANK], U8, align_bytes=64)
+        wqb_scales = consts.tile([P, 2 * HALF_COLS], U8, align_bytes=64)
+        nc.vector.memset(wqa_scales[:].bitcast(I32), 0)
+        nc.vector.memset(wqb_scales[:].bitcast(I32), 0)
+
+        pos_int = consts.tile([P, POS_PER_PART], I32)
+        nc.gpsimd.iota(pos_int[:], pattern=[[1, POS_PER_PART]], base=0, channel_multiplier=POS_PER_PART)
+        ident = consts.tile([P, P], F32)
+        masks.make_identity(nc, ident[:])
+        eps = consts.tile([P, 1], F32)
+        nc.gpsimd.memset(eps[:], EPS)
+
+        x_sb = [consts.tile([P, TILES, D_MODEL], BF16, name="x%d" % g) for g in range(N_GROUPS)]
+
+        def load_x(g):
+            b, w = divmod(g, GROUPS_PER_BATCH)
+            nc.sync.dma_start(out=x_sb[g][:], in_=x_view[b, :, TILES * w : TILES * (w + 1), :])
+
+        load_x(0)
+        wqa_codes = consts.tile([P, RANK], U32, align_bytes=64)
+        nc.sync.dma_start(
+            out=wqa_codes[:].bitcast(I32),
+            in_=Wqa_words.rearrange("g p n t -> (g p) (n t)").bitcast(I32),
+        )
+        for quad in range(4):
+            nc.sync.dma_start(
+                out=wqa_scales[32 * quad : 32 * quad + 4, :].bitcast(I32),
+                in_=Wqa_scales[0, 4 * quad : 4 * quad + 4, :].bitcast(I32),
+            )
+        gain = consts.tile([P, RANK], BF16)
+        nc.sync.dma_start(out=gain[:], in_=q_a_norm_w.partition_broadcast(P))
+        load_x(1)
+        wqb_codes = consts.tile([P, 2, HALF_COLS], U32, align_bytes=64)
+        wqb_words_src = (
+            Wqb_words.rearrange("g p n t -> (g p) (n t)")
+            .bitcast(I32)
+            .rearrange("p (h half d) -> p half h d", half=2, d=D_NOPE)
+        )
+        wqb_scales_src = Wqb_scales[0].bitcast(I32).rearrange(
+            "q (h half d) -> q half h d", half=2, d=D_NOPE // 4
+        )
+        wqb_scales_dst = wqb_scales[:].bitcast(I32).rearrange(
+            "p (half h d) -> p half h d", half=2, d=D_NOPE // 4
+        )
+        for half in range(2):
+            nc.sync.dma_start(
+                out=wqb_codes[:, half, :].bitcast(I32).rearrange("p (h d) -> p h d", d=D_NOPE),
+                in_=wqb_words_src[:, half],
+            )
+        for half in range(2):
+            for quad in range(4):
+                nc.sync.dma_start(
+                    out=wqb_scales_dst[32 * quad : 32 * quad + 4, half],
+                    in_=wqb_scales_src[4 * quad : 4 * quad + 4, half],
+                )
+        for g in range(2, N_GROUPS):
+            load_x(g)
+
+        def transpose_words(src, bank):
+            words = src[:].bitcast(F32)
+            for j in range(TILES):
+                for u in range(2):
+                    nc.tensor.transpose(bank[:, j, u, :], words[:, j, u:WORDS:2], ident[:])
+
+        def regroup(bank, name):
+            grouped = work.tile([P, TILES, P, 4], BF16, name=name, align_bytes=64)
+            nc.scalar.copy(out=grouped[:].bitcast(F32), in_=bank[:].rearrange("p j u r -> p j r u"))
+            return grouped
+
+        def quantise(grouped, name):
+            codes = work.tile([P, TILES * P], U32, name=name + "_codes", align_bytes=64)
+            scales = work.tile([P, TILES * P], U8, name=name + "_scales", align_bytes=64)
+            nc.vector.quantize_mx(
+                out=codes[:].bitcast(FP8X4),
+                scales=scales[:],
+                in_=grouped[:].rearrange("p j r t -> p (j r t)"),
+            )
+            return codes, scales
+
+        def mx_pass(acc, tokens, j, w_codes, w_scales):
+            codes, scales = tokens
+            cols = slice(j * P, (j + 1) * P)
+            nc.tensor.matmul_mx(
+                out=acc[:],
+                lhsT=codes[:, cols].bitcast(FP8X4),
+                lhsT_scale=scales[:, cols],
+                rhs=w_codes.bitcast(FP8X4),
+                rhs_scale=w_scales,
+                start=True,
+                stop=True,
+            )
+
+        x_grouped, x_mx, c_acc, std, h_grouped, h_mx, q_rope, result = {}, {}, {}, {}, {}, {}, {}, {}
+
+        def transpose_x(g):
+            x_t = psum_t.tile([P, TILES, 2, P], F32, name="x_t")
+            transpose_words(x_sb[g], x_t)
+            x_grouped[g] = regroup(x_t, "x_grouped")
+
+        def quantise_x(g):
+            x_mx[g] = quantise(x_grouped[g], "x")
+
+        def first_matmul(g):
+            sumsq = work.tile([P, TILES], F32, name="sumsq")
+            c_acc[g] = []
+            for j in range(TILES):
+                acc = psum_mm.tile([P, RANK], F32, name="c_acc")
+                mx_pass(acc, x_mx[g], j, wqa_codes[:], wqa_scales[:])
+                c_acc[g].append(acc)
+            for j in range(TILES):
+                squares = work.tile([P, RANK], BF16, name="squares")
+                nc.scalar.activation(
+                    out=squares[:], in_=c_acc[g][j][:], func=ACT.Square, accum_out=sumsq[:, j : j + 1]
+                )
+            std[g] = work.tile([P, TILES], F32, name="std")
+            nc.scalar.activation(out=std[g][:], in_=sumsq[:], func=ACT.Sqrt, scale=1.0 / RANK, bias=eps[:])
+
+        def normalise(g):
+            rstd = work.tile([P, TILES], F32, name="rstd")
+            nc.vector.reciprocal(out=rstd[:], in_=std[g][:])
+            h = work.tile([P, TILES, RANK], BF16, name="h")
+            for j in range(TILES):
+                nc.vector.scalar_tensor_tensor(
+                    out=h[:, j, :],
+                    in0=c_acc[g][j][:],
+                    scalar=rstd[:, j : j + 1],
+                    in1=gain[:],
+                    op0=ALU.mult,
+                    op1=ALU.mult,
+                )
+            return h
+
+        def transpose_h(g, h):
+            h_t = psum_t.tile([P, TILES, 2, P], F32, name="h_t")
+            transpose_words(h, h_t)
+            h_grouped[g] = regroup(h_t, "h_grouped")
+
+        def quantise_h(g):
+            h_mx[g] = quantise(h_grouped[g], "h")
+
+        def second_matmul(g, j):
+            if j == 0:
+                result[g] = outs.tile([P, HEADS, TILES, D_NOPE + D_ROPE], F32, name="result")
+                q_rope[g] = []
+            q_nope = psum_mm.tile([P, HALF_COLS], F32, name="q_nope")
+            q_rope[g].append(psum_mm.tile([P, HALF_COLS], F32, name="q_rope"))
+            mx_pass(q_nope, h_mx[g], j, wqb_codes[:, 0, :], wqb_scales[:, 0:HALF_COLS])
+            mx_pass(q_rope[g][j], h_mx[g], j, wqb_codes[:, 1, :], wqb_scales[:, HALF_COLS : 2 * HALF_COLS])
+            nc.scalar.copy(
+                out=result[g][:, :, j, 0:D_NOPE], in_=q_nope[:].rearrange("p (h d) -> p h d", d=D_NOPE)
+            )
+
+        def rotate(g, j):
+            t = TILES * (g % GROUPS_PER_BATCH) + j
+            shape = [P, 2, 2, HEADS * 2, PAIRS]
+            products = outs.tile([P, 2, 2, HEADS * N_ANGLES], F32, name="products")
+            nc.vector.tensor_tensor(
+                out=products[:].rearrange("p o e (hr i) -> p o e hr i", i=PAIRS),
+                in0=q_rope[g][j][:]
+                .rearrange("p (hr i e) -> p e hr i", e=2, i=PAIRS)
+                .unsqueeze(1)
+                .to_broadcast(shape),
+                in1=rot[:, t].unsqueeze(3).to_broadcast(shape),
+                op=ALU.mult,
+            )
+            nc.gpsimd.tensor_tensor(
+                out=result[g][:, :, j, D_NOPE:].rearrange("p h (i o) -> p h i o", o=2),
+                in0=products[:, :, 0, :].rearrange("p o (h i) -> p h i o", h=HEADS),
+                in1=products[:, :, 1, :].rearrange("p o (h i) -> p h i o", h=HEADS),
+                op=ALU.add,
+            )
+
+        def store(g):
+            b, w = divmod(g, GROUPS_PER_BATCH)
+            nc.sync.dma_start(out=out_view[b, :, :, TILES * w : TILES * (w + 1), :], in_=result[g][:])
+
+        pos = consts.tile([P, POS_PER_PART], F32)
+        nc.vector.tensor_copy(out=pos[:], in_=pos_int[:])
+        turns = consts.tile([P, N_ANGLES, POS_PER_PART], F32)
+        nc.vector.tensor_scalar(
+            out=turns[:, 0, :], in0=pos[:], scalar1=1.0 / (2.0 * math.pi), scalar2=None, op0=ALU.mult
+        )
+        for n in (1, 2, 4, 8, 16):
+            nc.vector.tensor_scalar(
+                out=turns[:, n : 2 * n, :],
+                in0=turns[:, 0:n, :],
+                scalar1=THETA ** (-n / N_ANGLES),
+                scalar2=None,
+                op0=ALU.mult,
+            )
+        turns_by_parity = turns[:].rearrange("p (i o) t -> p o t i", o=2)
+        shifted = consts.tile([P, POS_PER_PART, 2, 2, PAIRS], F32)
+        for o, e, sign, quarter in ((0, 0, 1.0, 0.25), (0, 1, -1.0, 0.0), (1, 0, 1.0, 0.0), (1, 1, 1.0, 0.25)):
+            nc.vector.tensor_scalar(
+                out=shifted[:, :, o, e, :],
+                in0=turns_by_parity[:, o],
+                scalar1=sign,
+                scalar2=quarter,
+                op0=ALU.mult,
+                op1=ALU.add,
+            )
+        whole = consts.tile([P, POS_PER_PART, 2, 2, PAIRS], F32)
+        nc.vector.tensor_scalar(
+            out=whole[:], in0=shifted[:], scalar1=ROUND_MAGIC, scalar2=ROUND_MAGIC, op0=ALU.add, op1=ALU.subtract
+        )
+        nc.vector.tensor_tensor(out=shifted[:], in0=shifted[:], in1=whole[:], op=ALU.subtract)
+
+        transpose_x(0)
+        rot = consts.tile([P, POS_PER_PART, 2, 2, PAIRS], F32)
+        nc.scalar.activation(out=rot[:], in_=shifted[:], func=ACT.Sin, scale=2.0 * math.pi)
+
+        def live(g):
+            return 0 <= g < N_GROUPS
+
+        for i in range(-1, N_GROUPS + 3):
+            if live(i - 1):
+                h = normalise(i - 1)
+            if live(i):
+                first_matmul(i)
+            if live(i - 1):
+                transpose_h(i - 1, h)
+            if live(i - 2):
+                quantise_h(i - 2)
+            if live(i + 2):
+                transpose_x(i + 2)
+            if live(i + 1):
+                quantise_x(i + 1)
+            for j in range(TILES):
+                if live(i - 3):
+                    rotate(i - 3, j)
+                if live(i - 2):
+                    second_matmul(i - 2, j)
+            if live(i - 3):
+                store(i - 3)

@@ -45,8 +45,8 @@ def tile_multiheadlatentattention_pa_t_kernel(
         consts = ctx.enter_context(tc.tile_pool(name="consts", bufs=1))
         work = ctx.enter_context(tc.tile_pool(name="work", bufs=2))
         outs = ctx.enter_context(tc.tile_pool(name="outs", bufs=3))
-        psum_t = ctx.enter_context(tc.psum_pool(name="psum_t", bufs=1))
-        psum_mm = ctx.enter_context(tc.psum_pool(name="psum_mm", bufs=TILES))
+        psum_front = ctx.enter_context(tc.psum_pool(name="psum_front", bufs=4))
+        psum_q = ctx.enter_context(tc.psum_pool(name="psum_q", bufs=TILES))
         ctx.enter_context(tc.manual_schedule())
 
         wqa_scales = consts.tile([P, RANK], U8, align_bytes=64)
@@ -60,6 +60,8 @@ def tile_multiheadlatentattention_pa_t_kernel(
         masks.make_identity(nc, ident[:])
         eps = consts.tile([P, 1], F32)
         nc.gpsimd.memset(eps[:], EPS)
+        warm = consts.tile([P, 1], F32)
+        nc.scalar.activation(out=warm[:], in_=eps[:], func=ACT.Sin)
 
         x_sb = [consts.tile([P, TILES, D_MODEL], BF16, name="x%d" % g) for g in range(N_GROUPS)]
 
@@ -144,7 +146,7 @@ def tile_multiheadlatentattention_pa_t_kernel(
         x_grouped, x_mx, c_acc, std, h_grouped, h_mx, q_rope, result = {}, {}, {}, {}, {}, {}, {}, {}
 
         def transpose_x(g):
-            x_t = psum_t.tile([P, TILES, 2, P], F32, name="x_t")
+            x_t = psum_front.tile([P, TILES, 2, P], F32, name="x_t", tag="front")
             transpose_words(x_sb[g], x_t)
             x_grouped[g] = regroup(x_t, "x_grouped")
 
@@ -155,7 +157,7 @@ def tile_multiheadlatentattention_pa_t_kernel(
             sumsq = work.tile([P, TILES], F32, name="sumsq")
             c_acc[g] = []
             for j in range(TILES):
-                acc = psum_mm.tile([P, RANK], F32, name="c_acc")
+                acc = psum_front.tile([P, RANK], F32, name="c_acc", tag="front")
                 mx_pass(acc, x_mx[g], j, wqa_codes[:], wqa_scales[:])
                 c_acc[g].append(acc)
             for j in range(TILES):
@@ -182,7 +184,7 @@ def tile_multiheadlatentattention_pa_t_kernel(
             return h
 
         def transpose_h(g, h):
-            h_t = psum_t.tile([P, TILES, 2, P], F32, name="h_t")
+            h_t = psum_front.tile([P, TILES, 2, P], F32, name="h_t", tag="front")
             transpose_words(h, h_t)
             h_grouped[g] = regroup(h_t, "h_grouped")
 
@@ -193,8 +195,8 @@ def tile_multiheadlatentattention_pa_t_kernel(
             if j == 0:
                 result[g] = outs.tile([P, HEADS, TILES, D_NOPE + D_ROPE], F32, name="result")
                 q_rope[g] = []
-            q_nope = psum_mm.tile([P, HALF_COLS], F32, name="q_nope")
-            q_rope[g].append(psum_mm.tile([P, HALF_COLS], F32, name="q_rope"))
+            q_nope = psum_q.tile([P, HALF_COLS], F32, name="q_nope")
+            q_rope[g].append(psum_q.tile([P, HALF_COLS], F32, name="q_rope"))
             mx_pass(q_nope, h_mx[g], j, wqb_codes[:, 0, :], wqb_scales[:, 0:HALF_COLS])
             mx_pass(q_rope[g][j], h_mx[g], j, wqb_codes[:, 1, :], wqb_scales[:, HALF_COLS : 2 * HALF_COLS])
             nc.scalar.copy(
@@ -203,21 +205,21 @@ def tile_multiheadlatentattention_pa_t_kernel(
 
         def rotate(g, j):
             t = TILES * (g % GROUPS_PER_BATCH) + j
-            shape = [P, 2, 2, HEADS * 2, PAIRS]
-            products = outs.tile([P, 2, 2, HEADS * N_ANGLES], F32, name="products")
+            shape = [P, 2, HEADS * 2, PAIRS, 2]
+            terms = outs.tile([P, 2, HALF_COLS], F32, name="terms")
             nc.vector.tensor_tensor(
-                out=products[:].rearrange("p o e (hr i) -> p o e hr i", i=PAIRS),
+                out=terms[:].rearrange("p e (hr i o) -> p e hr i o", i=PAIRS, o=2),
                 in0=q_rope[g][j][:]
                 .rearrange("p (hr i e) -> p e hr i", e=2, i=PAIRS)
-                .unsqueeze(1)
+                .unsqueeze(4)
                 .to_broadcast(shape),
-                in1=rot[:, t].unsqueeze(3).to_broadcast(shape),
+                in1=rot[:, t].unsqueeze(2).to_broadcast(shape),
                 op=ALU.mult,
             )
             nc.gpsimd.tensor_tensor(
-                out=result[g][:, :, j, D_NOPE:].rearrange("p h (i o) -> p h i o", o=2),
-                in0=products[:, :, 0, :].rearrange("p o (h i) -> p h i o", h=HEADS),
-                in1=products[:, :, 1, :].rearrange("p o (h i) -> p h i o", h=HEADS),
+                out=result[g][:, :, j, D_NOPE:],
+                in0=terms[:, 0, :].rearrange("p (h d) -> p h d", d=D_ROPE),
+                in1=terms[:, 1, :].rearrange("p (h d) -> p h d", d=D_ROPE),
                 op=ALU.add,
             )
 
@@ -240,24 +242,24 @@ def tile_multiheadlatentattention_pa_t_kernel(
                 op0=ALU.mult,
             )
         turns_by_parity = turns[:].rearrange("p (i o) t -> p o t i", o=2)
-        shifted = consts.tile([P, POS_PER_PART, 2, 2, PAIRS], F32)
-        for o, e, sign, quarter in ((0, 0, 1.0, 0.25), (0, 1, -1.0, 0.0), (1, 0, 1.0, 0.0), (1, 1, 1.0, 0.25)):
+        shifted = consts.tile([P, POS_PER_PART, 2, PAIRS, 2], F32)
+        for e, o, sign, quarter in ((0, 0, 1.0, 0.25), (0, 1, 1.0, 0.0), (1, 0, -1.0, 0.0), (1, 1, 1.0, 0.25)):
             nc.vector.tensor_scalar(
-                out=shifted[:, :, o, e, :],
+                out=shifted[:, :, e, :, o],
                 in0=turns_by_parity[:, o],
                 scalar1=sign,
                 scalar2=quarter,
                 op0=ALU.mult,
                 op1=ALU.add,
             )
-        whole = consts.tile([P, POS_PER_PART, 2, 2, PAIRS], F32)
+        whole = consts.tile([P, POS_PER_PART, 2, PAIRS, 2], F32)
         nc.vector.tensor_scalar(
             out=whole[:], in0=shifted[:], scalar1=ROUND_MAGIC, scalar2=ROUND_MAGIC, op0=ALU.add, op1=ALU.subtract
         )
         nc.vector.tensor_tensor(out=shifted[:], in0=shifted[:], in1=whole[:], op=ALU.subtract)
 
         transpose_x(0)
-        rot = consts.tile([P, POS_PER_PART, 2, 2, PAIRS], F32)
+        rot = consts.tile([P, POS_PER_PART, 2, PAIRS, 2], F32)
         nc.scalar.activation(out=rot[:], in_=shifted[:], func=ACT.Sin, scale=2.0 * math.pi)
 
         def live(g):

@@ -58,10 +58,10 @@ def tile_multiheadlatentattention_pa_t_kernel(
         nc.gpsimd.iota(pos_int[:], pattern=[[1, POS_PER_PART]], base=0, channel_multiplier=POS_PER_PART)
         ident = consts.tile([P, P], F32)
         masks.make_identity(nc, ident[:])
-        eps = consts.tile([P, 1], F32)
-        nc.gpsimd.memset(eps[:], EPS)
+        minus_half = consts.tile([P, TILES], F32)
+        nc.gpsimd.memset(minus_half[:], -0.5)
         warm = consts.tile([P, 1], F32)
-        nc.scalar.activation(out=warm[:], in_=eps[:], func=ACT.Sin)
+        nc.scalar.activation(out=warm[:], in_=minus_half[:, 0:1], func=ACT.Sin)
 
         x_sb = [consts.tile([P, TILES, D_MODEL], BF16, name="x%d" % g) for g in range(N_GROUPS)]
 
@@ -143,7 +143,7 @@ def tile_multiheadlatentattention_pa_t_kernel(
                 stop=True,
             )
 
-        x_grouped, x_mx, c_acc, std, h_grouped, h_mx, q_rope, result = {}, {}, {}, {}, {}, {}, {}, {}
+        x_grouped, x_mx, c_acc, rstd, h_grouped, h_mx, q_rope, result = {}, {}, {}, {}, {}, {}, {}, {}
 
         def transpose_x(g):
             x_t = psum_front.tile([P, TILES, 2, P], F32, name="x_t", tag="front")
@@ -165,18 +165,20 @@ def tile_multiheadlatentattention_pa_t_kernel(
                 nc.scalar.activation(
                     out=squares[:], in_=c_acc[g][j][:], func=ACT.Square, accum_out=sumsq[:, j : j + 1]
                 )
-            std[g] = work.tile([P, TILES], F32, name="std")
-            nc.scalar.activation(out=std[g][:], in_=sumsq[:], func=ACT.Sqrt, scale=1.0 / RANK, bias=eps[:])
+            mean = work.tile([P, TILES], F32, name="mean")
+            nc.gpsimd.tensor_scalar(
+                out=mean[:], in0=sumsq[:], scalar1=1.0 / RANK, scalar2=EPS, op0=ALU.mult, op1=ALU.add
+            )
+            rstd[g] = work.tile([P, TILES], F32, name="rstd")
+            nc.gpsimd.tensor_tensor(out=rstd[g][:], in0=mean[:], in1=minus_half[:], op=ALU.pow)
 
         def normalise(g):
-            rstd = work.tile([P, TILES], F32, name="rstd")
-            nc.vector.reciprocal(out=rstd[:], in_=std[g][:])
             h = work.tile([P, TILES, RANK], BF16, name="h")
             for j in range(TILES):
                 nc.vector.scalar_tensor_tensor(
                     out=h[:, j, :],
                     in0=c_acc[g][j][:],
-                    scalar=rstd[:, j : j + 1],
+                    scalar=rstd[g][:, j : j + 1],
                     in1=gain[:],
                     op0=ALU.mult,
                     op1=ALU.mult,

@@ -44,7 +44,7 @@ def tile_multiheadlatentattention_pa_t_kernel(
     with ExitStack() as ctx:
         consts = ctx.enter_context(tc.tile_pool(name="consts", bufs=1))
         work = ctx.enter_context(tc.tile_pool(name="work", bufs=2))
-        outs = ctx.enter_context(tc.tile_pool(name="outs", bufs=3))
+        outs = ctx.enter_context(tc.tile_pool(name="outs", bufs=2 * TILES))
         psum_front = ctx.enter_context(tc.psum_pool(name="psum_front", bufs=4))
         psum_q = ctx.enter_context(tc.psum_pool(name="psum_q", bufs=TILES))
         ctx.enter_context(tc.manual_schedule())
@@ -58,10 +58,15 @@ def tile_multiheadlatentattention_pa_t_kernel(
         nc.gpsimd.iota(pos_int[:], pattern=[[1, POS_PER_PART]], base=0, channel_multiplier=POS_PER_PART)
         ident = consts.tile([P, P], F32)
         masks.make_identity(nc, ident[:])
-        minus_half = consts.tile([P, TILES], F32)
-        nc.gpsimd.memset(minus_half[:], -0.5)
+        eps = consts.tile([P, 1], F32)
+        nc.gpsimd.memset(eps[:], EPS)
         warm = consts.tile([P, 1], F32)
-        nc.scalar.activation(out=warm[:], in_=minus_half[:, 0:1], func=ACT.Sin)
+        nc.scalar.activation(out=warm[:], in_=eps[:], func=ACT.Sin)
+
+        gain_row = consts.tile([P, RANK], BF16)
+        nc.vector.memset(gain_row[:], 0.0)
+        ones = consts.tile([P, P], BF16)
+        nc.vector.memset(ones[:], 1.0)
 
         x_sb = [consts.tile([P, TILES, D_MODEL], BF16, name="x%d" % g) for g in range(N_GROUPS)]
 
@@ -80,9 +85,10 @@ def tile_multiheadlatentattention_pa_t_kernel(
                 out=wqa_scales[32 * quad : 32 * quad + 4, :].bitcast(I32),
                 in_=Wqa_scales[0, 4 * quad : 4 * quad + 4, :].bitcast(I32),
             )
-        gain = consts.tile([P, RANK], BF16)
-        nc.sync.dma_start(out=gain[:], in_=q_a_norm_w.partition_broadcast(P))
         load_x(1)
+        load_x(2)
+        nc.sync.dma_start(out=gain_row[0:1, :], in_=q_a_norm_w.unsqueeze(0))
+        load_x(3)
         wqb_codes = consts.tile([P, 2, HALF_COLS], U32, align_bytes=64)
         wqb_words_src = (
             Wqb_words.rearrange("g p n t -> (g p) (n t)")
@@ -100,17 +106,19 @@ def tile_multiheadlatentattention_pa_t_kernel(
                 out=wqb_codes[:, half, :].bitcast(I32).rearrange("p (h d) -> p h d", d=D_NOPE),
                 in_=wqb_words_src[:, half],
             )
+        load_x(4)
+        load_x(5)
         for half in range(2):
             for quad in range(4):
                 nc.sync.dma_start(
                     out=wqb_scales_dst[32 * quad : 32 * quad + 4, half],
                     in_=wqb_scales_src[4 * quad : 4 * quad + 4, half],
                 )
-        for g in range(2, N_GROUPS):
+        for g in range(6, N_GROUPS):
             load_x(g)
 
         def transpose_words(src, bank):
-            words = src[:].bitcast(F32)
+            words = src.bitcast(F32)
             for j in range(TILES):
                 for u in range(2):
                     nc.tensor.transpose(bank[:, j, u, :], words[:, j, u:WORDS:2], ident[:])
@@ -143,11 +151,13 @@ def tile_multiheadlatentattention_pa_t_kernel(
                 stop=True,
             )
 
-        x_grouped, x_mx, c_acc, rstd, h_grouped, h_mx, q_rope, result = {}, {}, {}, {}, {}, {}, {}, {}
+        x_grouped, x_mx, c_acc, std, rstd, h_grouped, h_mx = {}, {}, {}, {}, {}, {}, {}
+        q_rope, terms, result = {}, {}, {}
+        held = consts.tile([P, 1], F32)
 
         def transpose_x(g):
             x_t = psum_front.tile([P, TILES, 2, P], F32, name="x_t", tag="front")
-            transpose_words(x_sb[g], x_t)
+            transpose_words(x_sb[g][:], x_t)
             x_grouped[g] = regroup(x_t, "x_grouped")
 
         def quantise_x(g):
@@ -165,12 +175,12 @@ def tile_multiheadlatentattention_pa_t_kernel(
                 nc.scalar.activation(
                     out=squares[:], in_=c_acc[g][j][:], func=ACT.Square, accum_out=sumsq[:, j : j + 1]
                 )
-            mean = work.tile([P, TILES], F32, name="mean")
-            nc.gpsimd.tensor_scalar(
-                out=mean[:], in0=sumsq[:], scalar1=1.0 / RANK, scalar2=EPS, op0=ALU.mult, op1=ALU.add
-            )
+            std[g] = work.tile([P, TILES], F32, name="std")
+            nc.scalar.activation(out=std[g][:], in_=sumsq[:], func=ACT.Sqrt, scale=1.0 / RANK, bias=eps[:])
+
+        def invert_std(g):
             rstd[g] = work.tile([P, TILES], F32, name="rstd")
-            nc.gpsimd.tensor_tensor(out=rstd[g][:], in0=mean[:], in1=minus_half[:], op=ALU.pow)
+            nc.vector.reciprocal(out=rstd[g][:], in_=std[g][:])
 
         def normalise(g):
             h = work.tile([P, TILES, RANK], BF16, name="h")
@@ -187,7 +197,7 @@ def tile_multiheadlatentattention_pa_t_kernel(
 
         def transpose_h(g, h):
             h_t = psum_front.tile([P, TILES, 2, P], F32, name="h_t", tag="front")
-            transpose_words(h, h_t)
+            transpose_words(h[:], h_t)
             h_grouped[g] = regroup(h_t, "h_grouped")
 
         def quantise_h(g):
@@ -205,12 +215,14 @@ def tile_multiheadlatentattention_pa_t_kernel(
                 out=result[g][:, :, j, 0:D_NOPE], in_=q_nope[:].rearrange("p (h d) -> p h d", d=D_NOPE)
             )
 
-        def rotate(g, j):
+        def rotate_terms(g, j):
             t = TILES * (g % GROUPS_PER_BATCH) + j
             shape = [P, 2, HEADS * 2, PAIRS, 2]
-            terms = outs.tile([P, 2, HALF_COLS], F32, name="terms")
+            if j == 0:
+                terms[g] = []
+            terms[g].append(outs.tile([P, 2, HALF_COLS], F32, name="terms"))
             nc.vector.tensor_tensor(
-                out=terms[:].rearrange("p e (hr i o) -> p e hr i o", i=PAIRS, o=2),
+                out=terms[g][j][:].rearrange("p e (hr i o) -> p e hr i o", i=PAIRS, o=2),
                 in0=q_rope[g][j][:]
                 .rearrange("p (hr i e) -> p e hr i", e=2, i=PAIRS)
                 .unsqueeze(4)
@@ -218,10 +230,15 @@ def tile_multiheadlatentattention_pa_t_kernel(
                 in1=rot[:, t].unsqueeze(2).to_broadcast(shape),
                 op=ALU.mult,
             )
+
+        def hold_gpsimd_for(codes):
+            nc.gpsimd.tensor_copy(out=held[:], in_=codes[:, 0:1].bitcast(F32))
+
+        def add_terms(g, j):
             nc.gpsimd.tensor_tensor(
                 out=result[g][:, :, j, D_NOPE:],
-                in0=terms[:, 0, :].rearrange("p (h d) -> p h d", d=D_ROPE),
-                in1=terms[:, 1, :].rearrange("p (h d) -> p h d", d=D_ROPE),
+                in0=terms[g][j][:, 0, :].rearrange("p (h d) -> p h d", d=D_ROPE),
+                in1=terms[g][j][:, 1, :].rearrange("p (h d) -> p h d", d=D_ROPE),
                 op=ALU.add,
             )
 
@@ -261,13 +278,17 @@ def tile_multiheadlatentattention_pa_t_kernel(
         nc.vector.tensor_tensor(out=shifted[:], in0=shifted[:], in1=whole[:], op=ALU.subtract)
 
         transpose_x(0)
+        gain_acc = psum_front.tile([P, RANK], F32, name="gain_acc", tag="front")
+        nc.tensor.matmul(out=gain_acc[:], lhsT=ones[:], rhs=gain_row[:], start=True, stop=True)
+        gain = consts.tile([P, RANK], F32)
+        nc.vector.tensor_copy(out=gain[:], in_=gain_acc[:])
         rot = consts.tile([P, POS_PER_PART, 2, PAIRS, 2], F32)
         nc.scalar.activation(out=rot[:], in_=shifted[:], func=ACT.Sin, scale=2.0 * math.pi)
 
         def live(g):
             return 0 <= g < N_GROUPS
 
-        for i in range(-1, N_GROUPS + 3):
+        for i in range(-1, N_GROUPS + 4):
             if live(i - 1):
                 h = normalise(i - 1)
             if live(i):
@@ -280,10 +301,19 @@ def tile_multiheadlatentattention_pa_t_kernel(
                 transpose_x(i + 2)
             if live(i + 1):
                 quantise_x(i + 1)
+            if live(i - 4):
+                if live(i + 1):
+                    hold_gpsimd_for(x_mx[i + 1][0])
+                elif live(i - 2):
+                    hold_gpsimd_for(h_mx[i - 2][0])
+                add_terms(i - 4, TILES - 1)
+                store(i - 4)
             for j in range(TILES):
                 if live(i - 3):
-                    rotate(i - 3, j)
+                    rotate_terms(i - 3, j)
+                    if j < TILES - 1:
+                        add_terms(i - 3, j)
                 if live(i - 2):
                     second_matmul(i - 2, j)
-            if live(i - 3):
-                store(i - 3)
+                if j == 0 and live(i):
+                    invert_std(i)

@@ -45,6 +45,7 @@ def tile_multiheadlatentattention_pa_t_kernel(
         consts = ctx.enter_context(tc.tile_pool(name="consts", bufs=1))
         work = ctx.enter_context(tc.tile_pool(name="work", bufs=2))
         outs = ctx.enter_context(tc.tile_pool(name="outs", bufs=2 * TILES))
+        results = ctx.enter_context(tc.tile_pool(name="results", bufs=4 * TILES))
         psum_front = ctx.enter_context(tc.psum_pool(name="psum_front", bufs=4))
         psum_q = ctx.enter_context(tc.psum_pool(name="psum_q", bufs=TILES))
         ctx.enter_context(tc.manual_schedule())
@@ -151,7 +152,7 @@ def tile_multiheadlatentattention_pa_t_kernel(
                 stop=True,
             )
 
-        x_grouped, x_mx, c_acc, std, rstd, h_grouped, h_mx = {}, {}, {}, {}, {}, {}, {}
+        x_grouped, x_mx, c_acc, rstd, h_grouped, h_mx = {}, {}, {}, {}, {}, {}
         q_rope, terms, result = {}, {}, {}
         held = consts.tile([P, 1], F32)
 
@@ -175,12 +176,10 @@ def tile_multiheadlatentattention_pa_t_kernel(
                 nc.scalar.activation(
                     out=squares[:], in_=c_acc[g][j][:], func=ACT.Square, accum_out=sumsq[:, j : j + 1]
                 )
-            std[g] = work.tile([P, TILES], F32, name="std")
-            nc.scalar.activation(out=std[g][:], in_=sumsq[:], func=ACT.Sqrt, scale=1.0 / RANK, bias=eps[:])
-
-        def invert_std(g):
             rstd[g] = work.tile([P, TILES], F32, name="rstd")
-            nc.vector.reciprocal(out=rstd[g][:], in_=std[g][:])
+            nc.scalar.activation(
+                out=rstd[g][:], in_=sumsq[:], func=ACT.Abs_reciprocal_sqrt, scale=1.0 / RANK, bias=eps[:]
+            )
 
         def normalise(g):
             h = work.tile([P, TILES, RANK], BF16, name="h")
@@ -205,14 +204,15 @@ def tile_multiheadlatentattention_pa_t_kernel(
 
         def second_matmul(g, j):
             if j == 0:
-                result[g] = outs.tile([P, HEADS, TILES, D_NOPE + D_ROPE], F32, name="result")
+                result[g] = []
                 q_rope[g] = []
+            result[g].append(results.tile([P, HEADS, D_NOPE + D_ROPE], F32, name="result"))
             q_nope = psum_q.tile([P, HALF_COLS], F32, name="q_nope")
             q_rope[g].append(psum_q.tile([P, HALF_COLS], F32, name="q_rope"))
             mx_pass(q_nope, h_mx[g], j, wqb_codes[:, 0, :], wqb_scales[:, 0:HALF_COLS])
             mx_pass(q_rope[g][j], h_mx[g], j, wqb_codes[:, 1, :], wqb_scales[:, HALF_COLS : 2 * HALF_COLS])
             nc.scalar.copy(
-                out=result[g][:, :, j, 0:D_NOPE], in_=q_nope[:].rearrange("p (h d) -> p h d", d=D_NOPE)
+                out=result[g][j][:, :, 0:D_NOPE], in_=q_nope[:].rearrange("p (h d) -> p h d", d=D_NOPE)
             )
 
         def rotate_terms(g, j):
@@ -234,17 +234,15 @@ def tile_multiheadlatentattention_pa_t_kernel(
         def hold_gpsimd_for(codes):
             nc.gpsimd.tensor_copy(out=held[:], in_=codes[:, 0:1].bitcast(F32))
 
-        def add_terms(g, j):
-            nc.gpsimd.tensor_tensor(
-                out=result[g][:, :, j, D_NOPE:],
+        def add_terms_and_store(engine, g, j):
+            engine.tensor_tensor(
+                out=result[g][j][:, :, D_NOPE:],
                 in0=terms[g][j][:, 0, :].rearrange("p (h d) -> p h d", d=D_ROPE),
                 in1=terms[g][j][:, 1, :].rearrange("p (h d) -> p h d", d=D_ROPE),
                 op=ALU.add,
             )
-
-        def store(g):
             b, w = divmod(g, GROUPS_PER_BATCH)
-            nc.sync.dma_start(out=out_view[b, :, :, TILES * w : TILES * (w + 1), :], in_=result[g][:])
+            nc.sync.dma_start(out=out_view[b, :, :, TILES * w + j, :], in_=result[g][j][:])
 
         pos = consts.tile([P, POS_PER_PART], F32)
         nc.vector.tensor_copy(out=pos[:], in_=pos_int[:])
@@ -306,14 +304,11 @@ def tile_multiheadlatentattention_pa_t_kernel(
                     hold_gpsimd_for(x_mx[i + 1][0])
                 elif live(i - 2):
                     hold_gpsimd_for(h_mx[i - 2][0])
-                add_terms(i - 4, TILES - 1)
-                store(i - 4)
+                add_terms_and_store(nc.gpsimd if live(i - 3) else nc.vector, i - 4, TILES - 1)
             for j in range(TILES):
                 if live(i - 3):
                     rotate_terms(i - 3, j)
                     if j < TILES - 1:
-                        add_terms(i - 3, j)
+                        add_terms_and_store(nc.gpsimd, i - 3, j)
                 if live(i - 2):
                     second_matmul(i - 2, j)
-                if j == 0 and live(i):
-                    invert_std(i)

@@ -53,6 +53,10 @@ def tile_multiheadlatentattention_pa_t_kernel(
         wqa_scales = consts.tile([P, RANK], U8, align_bytes=64)
         wqb_scales = consts.tile([P, 2 * HALF_COLS], U8, align_bytes=64)
         nc.vector.memset(wqa_scales[:].bitcast(I32), 0)
+        gain_row = consts.tile([P, RANK], BF16)
+        nc.vector.memset(gain_row[:], 0.0)
+        ones = consts.tile([P, P], BF16)
+        nc.vector.memset(ones[:], 1.0)
         nc.vector.memset(wqb_scales[:].bitcast(I32), 0)
 
         pos_int = consts.tile([P, POS_PER_PART], I32)
@@ -64,11 +68,6 @@ def tile_multiheadlatentattention_pa_t_kernel(
         warm = consts.tile([P, 1], F32)
         nc.scalar.activation(out=warm[:], in_=eps[:], func=ACT.Sin)
 
-        gain_row = consts.tile([P, RANK], BF16)
-        nc.vector.memset(gain_row[:], 0.0)
-        ones = consts.tile([P, P], BF16)
-        nc.vector.memset(ones[:], 1.0)
-
         x_sb = [consts.tile([P, TILES, D_MODEL], BF16, name="x%d" % g) for g in range(N_GROUPS)]
 
         def load_x(g):
@@ -76,6 +75,7 @@ def tile_multiheadlatentattention_pa_t_kernel(
             nc.sync.dma_start(out=x_sb[g][:], in_=x_view[b, :, TILES * w : TILES * (w + 1), :])
 
         load_x(0)
+        nc.sync.dma_start(out=gain_row[0:1, :], in_=q_a_norm_w.unsqueeze(0))
         wqa_codes = consts.tile([P, RANK], U32, align_bytes=64)
         nc.sync.dma_start(
             out=wqa_codes[:].bitcast(I32),
@@ -88,7 +88,6 @@ def tile_multiheadlatentattention_pa_t_kernel(
             )
         load_x(1)
         load_x(2)
-        nc.sync.dma_start(out=gain_row[0:1, :], in_=q_a_norm_w.unsqueeze(0))
         load_x(3)
         wqb_codes = consts.tile([P, 2, HALF_COLS], U32, align_bytes=64)
         wqb_words_src = (
@@ -152,7 +151,7 @@ def tile_multiheadlatentattention_pa_t_kernel(
                 stop=True,
             )
 
-        x_grouped, x_mx, c_acc, rstd, h_grouped, h_mx = {}, {}, {}, {}, {}, {}
+        x_grouped, x_mx, c_acc, sumsq, rstd, h_grouped, h_mx = {}, {}, {}, {}, {}, {}, {}
         q_rope, terms, result = {}, {}, {}
         held = consts.tile([P, 1], F32)
 
@@ -165,7 +164,7 @@ def tile_multiheadlatentattention_pa_t_kernel(
             x_mx[g] = quantise(x_grouped[g], "x")
 
         def first_matmul(g):
-            sumsq = work.tile([P, TILES], F32, name="sumsq")
+            sumsq[g] = work.tile([P, TILES], F32, name="sumsq")
             c_acc[g] = []
             for j in range(TILES):
                 acc = psum_front.tile([P, RANK], F32, name="c_acc", tag="front")
@@ -174,11 +173,13 @@ def tile_multiheadlatentattention_pa_t_kernel(
             for j in range(TILES):
                 squares = work.tile([P, RANK], BF16, name="squares")
                 nc.scalar.activation(
-                    out=squares[:], in_=c_acc[g][j][:], func=ACT.Square, accum_out=sumsq[:, j : j + 1]
+                    out=squares[:], in_=c_acc[g][j][:], func=ACT.Square, accum_out=sumsq[g][:, j : j + 1]
                 )
+
+        def inverse_norm(g):
             rstd[g] = work.tile([P, TILES], F32, name="rstd")
             nc.scalar.activation(
-                out=rstd[g][:], in_=sumsq[:], func=ACT.Abs_reciprocal_sqrt, scale=1.0 / RANK, bias=eps[:]
+                out=rstd[g][:], in_=sumsq[g][:], func=ACT.Abs_reciprocal_sqrt, scale=1.0 / RANK, bias=eps[:]
             )
 
         def normalise(g):
@@ -269,28 +270,35 @@ def tile_multiheadlatentattention_pa_t_kernel(
                 op0=ALU.mult,
                 op1=ALU.add,
             )
+
+        transpose_x(0)
+        gain_acc = psum_front.tile([P, RANK], F32, name="gain_acc", tag="front")
+        nc.tensor.matmul(out=gain_acc[:], lhsT=ones[:], rhs=gain_row[:], start=True, stop=True)
+        transpose_x(1)
+        quantise_x(0)
         whole = consts.tile([P, POS_PER_PART, 2, PAIRS, 2], F32)
         nc.vector.tensor_scalar(
             out=whole[:], in0=shifted[:], scalar1=ROUND_MAGIC, scalar2=ROUND_MAGIC, op0=ALU.add, op1=ALU.subtract
         )
         nc.vector.tensor_tensor(out=shifted[:], in0=shifted[:], in1=whole[:], op=ALU.subtract)
-
-        transpose_x(0)
-        gain_acc = psum_front.tile([P, RANK], F32, name="gain_acc", tag="front")
-        nc.tensor.matmul(out=gain_acc[:], lhsT=ones[:], rhs=gain_row[:], start=True, stop=True)
         gain = consts.tile([P, RANK], F32)
         nc.vector.tensor_copy(out=gain[:], in_=gain_acc[:])
+        first_matmul(0)
         rot = consts.tile([P, POS_PER_PART, 2, PAIRS, 2], F32)
         nc.scalar.activation(out=rot[:], in_=shifted[:], func=ACT.Sin, scale=2.0 * math.pi)
+        inverse_norm(0)
+        transpose_x(2)
+        quantise_x(1)
 
         def live(g):
             return 0 <= g < N_GROUPS
 
-        for i in range(-1, N_GROUPS + 4):
+        for i in range(1, N_GROUPS + 4):
             if live(i - 1):
                 h = normalise(i - 1)
             if live(i):
                 first_matmul(i)
+                inverse_norm(i)
             if live(i - 1):
                 transpose_h(i - 1, h)
             if live(i - 2):

@@ -28,6 +28,7 @@ N_GROUPS = BATCH * GROUPS_PER_BATCH
 WORDS = D_MODEL // 2
 
 N_ANGLES = D_ROPE // 2
+X_PART, H_PART = 0, 1
 PAIRS = N_ANGLES // 2
 ROUND_MAGIC = 1.5 * 2.0**23
 
@@ -45,7 +46,7 @@ def tile_multiheadlatentattention_pa_t_kernel(
         consts = ctx.enter_context(tc.tile_pool(name="consts", bufs=1))
         work = ctx.enter_context(tc.tile_pool(name="work", bufs=2))
         outs = ctx.enter_context(tc.tile_pool(name="outs", bufs=2 * TILES))
-        results = ctx.enter_context(tc.tile_pool(name="results", bufs=4 * TILES))
+        results = ctx.enter_context(tc.tile_pool(name="results", bufs=4))
         psum_front = ctx.enter_context(tc.psum_pool(name="psum_front", bufs=4))
         psum_q = ctx.enter_context(tc.psum_pool(name="psum_q", bufs=TILES))
         ctx.enter_context(tc.manual_schedule())
@@ -123,24 +124,29 @@ def tile_multiheadlatentattention_pa_t_kernel(
                 for u in range(2):
                     nc.tensor.transpose(bank[:, j, u, :], words[:, j, u:WORDS:2], ident[:])
 
-        def regroup(bank, name):
-            grouped = work.tile([P, TILES, P, 4], BF16, name=name, align_bytes=64)
-            nc.scalar.copy(out=grouped[:].bitcast(F32), in_=bank[:].rearrange("p j u r -> p j r u"))
-            return grouped
+        grouped_of_round = {}
 
-        def quantise(grouped, name):
-            codes = work.tile([P, TILES * P], U32, name=name + "_codes", align_bytes=64)
-            scales = work.tile([P, TILES * P], U8, name=name + "_scales", align_bytes=64)
+        def regroup(bank, rnd, part):
+            if rnd not in grouped_of_round:
+                grouped_of_round[rnd] = work.tile([P, 2, TILES, P, 4], BF16, name="grouped", align_bytes=64)
+            nc.scalar.copy(
+                out=grouped_of_round[rnd][:, part].bitcast(F32), in_=bank[:].rearrange("p j u r -> p j r u")
+            )
+
+        def quantise(rnd, parts):
+            codes = work.tile([P, 2 * TILES * P], U32, name="codes", align_bytes=64)
+            scales = work.tile([P, 2 * TILES * P], U8, name="scales", align_bytes=64)
+            cols = slice(parts[0] * TILES * P, (parts[-1] + 1) * TILES * P)
             nc.vector.quantize_mx(
-                out=codes[:].bitcast(FP8X4),
-                scales=scales[:],
-                in_=grouped[:].rearrange("p j r t -> p (j r t)"),
+                out=codes[:, cols].bitcast(FP8X4),
+                scales=scales[:, cols],
+                in_=grouped_of_round[rnd][:, parts[0] : parts[-1] + 1].rearrange("p a j r t -> p (a j r t)"),
             )
             return codes, scales
 
         def mx_pass(acc, tokens, j, w_codes, w_scales):
-            codes, scales = tokens
-            cols = slice(j * P, (j + 1) * P)
+            codes, scales, part = tokens
+            cols = slice((part * TILES + j) * P, (part * TILES + j + 1) * P)
             nc.tensor.matmul_mx(
                 out=acc[:],
                 lhsT=codes[:, cols].bitcast(FP8X4),
@@ -151,17 +157,20 @@ def tile_multiheadlatentattention_pa_t_kernel(
                 stop=True,
             )
 
-        x_grouped, x_mx, c_acc, sumsq, rstd, h_grouped, h_mx = {}, {}, {}, {}, {}, {}, {}
+        x_mx, c_acc, sumsq, rstd, h_mx = {}, {}, {}, {}, {}
         q_rope, terms, result = {}, {}, {}
         held = consts.tile([P, 1], F32)
 
         def transpose_x(g):
             x_t = psum_front.tile([P, TILES, 2, P], F32, name="x_t", tag="front")
             transpose_words(x_sb[g][:], x_t)
-            x_grouped[g] = regroup(x_t, "x_grouped")
+            regroup(x_t, g - 1, X_PART)
 
-        def quantise_x(g):
-            x_mx[g] = quantise(x_grouped[g], "x")
+        def quantise_round(rnd):
+            parts = [part for part, g in ((X_PART, rnd + 1), (H_PART, rnd - 2)) if 0 <= g < N_GROUPS]
+            codes, scales = quantise(rnd, parts)
+            x_mx[rnd + 1] = (codes, scales, X_PART)
+            h_mx[rnd - 2] = (codes, scales, H_PART)
 
         def first_matmul(g):
             sumsq[g] = work.tile([P, TILES], F32, name="sumsq")
@@ -198,22 +207,18 @@ def tile_multiheadlatentattention_pa_t_kernel(
         def transpose_h(g, h):
             h_t = psum_front.tile([P, TILES, 2, P], F32, name="h_t", tag="front")
             transpose_words(h[:], h_t)
-            h_grouped[g] = regroup(h_t, "h_grouped")
-
-        def quantise_h(g):
-            h_mx[g] = quantise(h_grouped[g], "h")
+            regroup(h_t, g + 2, H_PART)
 
         def second_matmul(g, j):
             if j == 0:
-                result[g] = []
                 q_rope[g] = []
-            result[g].append(results.tile([P, HEADS, D_NOPE + D_ROPE], F32, name="result"))
+                result[g] = results.tile([P, HEADS, TILES, D_NOPE + D_ROPE], F32, name="result")
             q_nope = psum_q.tile([P, HALF_COLS], F32, name="q_nope")
             q_rope[g].append(psum_q.tile([P, HALF_COLS], F32, name="q_rope"))
             mx_pass(q_nope, h_mx[g], j, wqb_codes[:, 0, :], wqb_scales[:, 0:HALF_COLS])
             mx_pass(q_rope[g][j], h_mx[g], j, wqb_codes[:, 1, :], wqb_scales[:, HALF_COLS : 2 * HALF_COLS])
             nc.scalar.copy(
-                out=result[g][j][:, :, 0:D_NOPE], in_=q_nope[:].rearrange("p (h d) -> p h d", d=D_NOPE)
+                out=result[g][:, :, j, 0:D_NOPE], in_=q_nope[:].rearrange("p (h d) -> p h d", d=D_NOPE)
             )
 
         def rotate_terms(g, j):
@@ -232,18 +237,23 @@ def tile_multiheadlatentattention_pa_t_kernel(
                 op=ALU.mult,
             )
 
-        def hold_gpsimd_for(codes):
-            nc.gpsimd.tensor_copy(out=held[:], in_=codes[:, 0:1].bitcast(F32))
+        def hold_gpsimd_for(tokens):
+            codes, scales, part = tokens
+            first = part * TILES * P
+            nc.gpsimd.tensor_copy(out=held[:], in_=codes[:, first : first + 1].bitcast(F32))
 
         def add_terms_and_store(engine, g, j):
             engine.tensor_tensor(
-                out=result[g][j][:, :, D_NOPE:],
+                out=result[g][:, :, j, D_NOPE:],
                 in0=terms[g][j][:, 0, :].rearrange("p (h d) -> p h d", d=D_ROPE),
                 in1=terms[g][j][:, 1, :].rearrange("p (h d) -> p h d", d=D_ROPE),
                 op=ALU.add,
             )
             b, w = divmod(g, GROUPS_PER_BATCH)
-            nc.sync.dma_start(out=out_view[b, :, :, TILES * w + j, :], in_=result[g][j][:])
+            if g == N_GROUPS - 1:
+                nc.sync.dma_start(out=out_view[b, :, :, TILES * w + j, :], in_=result[g][:, :, j, :])
+            elif j == TILES - 1:
+                nc.sync.dma_start(out=out_view[b, :, :, TILES * w : TILES * (w + 1), :], in_=result[g][:])
 
         pos = consts.tile([P, POS_PER_PART], F32)
         nc.vector.tensor_copy(out=pos[:], in_=pos_int[:])
@@ -275,7 +285,7 @@ def tile_multiheadlatentattention_pa_t_kernel(
         gain_acc = psum_front.tile([P, RANK], F32, name="gain_acc", tag="front")
         nc.tensor.matmul(out=gain_acc[:], lhsT=ones[:], rhs=gain_row[:], start=True, stop=True)
         transpose_x(1)
-        quantise_x(0)
+        quantise_round(-1)
         whole = consts.tile([P, POS_PER_PART, 2, PAIRS, 2], F32)
         nc.vector.tensor_scalar(
             out=whole[:], in0=shifted[:], scalar1=ROUND_MAGIC, scalar2=ROUND_MAGIC, op0=ALU.add, op1=ALU.subtract
@@ -288,7 +298,7 @@ def tile_multiheadlatentattention_pa_t_kernel(
         nc.scalar.activation(out=rot[:], in_=shifted[:], func=ACT.Sin, scale=2.0 * math.pi)
         inverse_norm(0)
         transpose_x(2)
-        quantise_x(1)
+        quantise_round(0)
 
         def live(g):
             return 0 <= g < N_GROUPS
@@ -301,17 +311,15 @@ def tile_multiheadlatentattention_pa_t_kernel(
                 inverse_norm(i)
             if live(i - 1):
                 transpose_h(i - 1, h)
-            if live(i - 2):
-                quantise_h(i - 2)
             if live(i + 2):
                 transpose_x(i + 2)
-            if live(i + 1):
-                quantise_x(i + 1)
+            if live(i + 1) or live(i - 2):
+                quantise_round(i)
             if live(i - 4):
                 if live(i + 1):
-                    hold_gpsimd_for(x_mx[i + 1][0])
+                    hold_gpsimd_for(x_mx[i + 1])
                 elif live(i - 2):
-                    hold_gpsimd_for(h_mx[i - 2][0])
+                    hold_gpsimd_for(h_mx[i - 2])
                 add_terms_and_store(nc.gpsimd if live(i - 3) else nc.vector, i - 4, TILES - 1)
             for j in range(TILES):
                 if live(i - 3):

@@ -54,18 +54,24 @@ def tile_multiheadlatentattention_pa_t_kernel(
         wqa_scales = consts.tile([P, RANK], U8, align_bytes=64)
         wqb_scales = consts.tile([P, 2 * HALF_COLS], U8, align_bytes=64)
         nc.vector.memset(wqa_scales[:].bitcast(I32), 0)
-        gain_row = consts.tile([P, RANK], BF16)
-        nc.vector.memset(gain_row[:], 0.0)
-        ones = consts.tile([P, P], BF16)
-        nc.vector.memset(ones[:], 1.0)
-        nc.vector.memset(wqb_scales[:].bitcast(I32), 0)
-
-        pos_int = consts.tile([P, POS_PER_PART], I32)
-        nc.gpsimd.iota(pos_int[:], pattern=[[1, POS_PER_PART]], base=0, channel_multiplier=POS_PER_PART)
+        eps = consts.tile([P, 1], F32)
+        nc.vector.memset(eps[:], EPS)
+        pos = consts.tile([P, POS_PER_PART], F32)
+        nc.gpsimd.iota(
+            pos[:],
+            pattern=[[1, POS_PER_PART]],
+            base=0,
+            channel_multiplier=POS_PER_PART,
+            allow_small_or_imprecise_dtypes=True,
+        )
         ident = consts.tile([P, P], F32)
         masks.make_identity(nc, ident[:])
-        eps = consts.tile([P, 1], F32)
-        nc.gpsimd.memset(eps[:], EPS)
+        gain_row = consts.tile([P, RANK], BF16)
+        nc.gpsimd.memset(gain_row[:], 0.0)
+        ones = consts.tile([P, P], BF16)
+        nc.gpsimd.memset(ones[:], 1.0)
+        nc.gpsimd.memset(wqb_scales[:].bitcast(I32), 0)
+
         warm = consts.tile([P, 1], F32)
         nc.scalar.activation(out=warm[:], in_=eps[:], func=ACT.Sin)
 
@@ -76,7 +82,6 @@ def tile_multiheadlatentattention_pa_t_kernel(
             nc.sync.dma_start(out=x_sb[g][:], in_=x_view[b, :, TILES * w : TILES * (w + 1), :])
 
         load_x(0)
-        nc.sync.dma_start(out=gain_row[0:1, :], in_=q_a_norm_w.unsqueeze(0))
         wqa_codes = consts.tile([P, RANK], U32, align_bytes=64)
         nc.sync.dma_start(
             out=wqa_codes[:].bitcast(I32),
@@ -87,6 +92,7 @@ def tile_multiheadlatentattention_pa_t_kernel(
                 out=wqa_scales[32 * quad : 32 * quad + 4, :].bitcast(I32),
                 in_=Wqa_scales[0, 4 * quad : 4 * quad + 4, :].bitcast(I32),
             )
+        nc.sync.dma_start(out=gain_row[0:1, :], in_=q_a_norm_w.unsqueeze(0))
         load_x(1)
         load_x(2)
         load_x(3)
@@ -126,12 +132,10 @@ def tile_multiheadlatentattention_pa_t_kernel(
 
         grouped_of_round = {}
 
-        def regroup(bank, rnd, part):
+        def regroup(bank, rnd, part, copy=nc.scalar.copy):
             if rnd not in grouped_of_round:
                 grouped_of_round[rnd] = work.tile([P, 2, TILES, P, 4], BF16, name="grouped", align_bytes=64)
-            nc.scalar.copy(
-                out=grouped_of_round[rnd][:, part].bitcast(F32), in_=bank[:].rearrange("p j u r -> p j r u")
-            )
+            copy(out=grouped_of_round[rnd][:, part].bitcast(F32), in_=bank[:].rearrange("p j u r -> p j r u"))
 
         def quantise(rnd, parts):
             codes = work.tile([P, 2 * TILES * P], U32, name="codes", align_bytes=64)
@@ -161,10 +165,10 @@ def tile_multiheadlatentattention_pa_t_kernel(
         q_rope, terms, result = {}, {}, {}
         held = consts.tile([P, 1], F32)
 
-        def transpose_x(g):
+        def transpose_x(g, copy=nc.scalar.copy):
             x_t = psum_front.tile([P, TILES, 2, P], F32, name="x_t", tag="front")
             transpose_words(x_sb[g][:], x_t)
-            regroup(x_t, g - 1, X_PART)
+            regroup(x_t, g - 1, X_PART, copy)
 
         def quantise_round(rnd):
             parts = [part for part, g in ((X_PART, rnd + 1), (H_PART, rnd - 2)) if 0 <= g < N_GROUPS]
@@ -172,11 +176,11 @@ def tile_multiheadlatentattention_pa_t_kernel(
             x_mx[rnd + 1] = (codes, scales, X_PART)
             h_mx[rnd - 2] = (codes, scales, H_PART)
 
-        def first_matmul(g):
+        def first_matmul(g, pool, tag):
             sumsq[g] = work.tile([P, TILES], F32, name="sumsq")
             c_acc[g] = []
             for j in range(TILES):
-                acc = psum_front.tile([P, RANK], F32, name="c_acc", tag="front")
+                acc = pool.tile([P, RANK], F32, name="c_acc", tag=tag)
                 mx_pass(acc, x_mx[g], j, wqa_codes[:], wqa_scales[:])
                 c_acc[g].append(acc)
             for j in range(TILES):
@@ -255,50 +259,56 @@ def tile_multiheadlatentattention_pa_t_kernel(
             elif j == TILES - 1:
                 nc.sync.dma_start(out=out_view[b, :, :, TILES * w : TILES * (w + 1), :], in_=result[g][:])
 
-        pos = consts.tile([P, POS_PER_PART], F32)
-        nc.vector.tensor_copy(out=pos[:], in_=pos_int[:])
-        turns = consts.tile([P, N_ANGLES, POS_PER_PART], F32)
-        nc.vector.tensor_scalar(
-            out=turns[:, 0, :], in0=pos[:], scalar1=1.0 / (2.0 * math.pi), scalar2=None, op0=ALU.mult
-        )
-        for n in (1, 2, 4, 8, 16):
+        turns = consts.tile([P, 2, N_ANGLES, POS_PER_PART], F32)
+        for n in range(4):
             nc.vector.tensor_scalar(
-                out=turns[:, n : 2 * n, :],
-                in0=turns[:, 0:n, :],
+                out=turns[:, 0, n, :],
+                in0=pos[:],
+                scalar1=THETA ** (-n / N_ANGLES) / (2.0 * math.pi),
+                scalar2=None,
+                op0=ALU.mult,
+            )
+        for n in (4, 8, 16):
+            nc.vector.tensor_scalar(
+                out=turns[:, 0, n : 2 * n, :],
+                in0=turns[:, 0, 0:n, :],
                 scalar1=THETA ** (-n / N_ANGLES),
                 scalar2=None,
                 op0=ALU.mult,
             )
-        turns_by_parity = turns[:].rearrange("p (i o) t -> p o t i", o=2)
-        shifted = consts.tile([P, POS_PER_PART, 2, PAIRS, 2], F32)
-        for e, o, sign, quarter in ((0, 0, 1.0, 0.25), (0, 1, 1.0, 0.0), (1, 0, -1.0, 0.0), (1, 1, 1.0, 0.25)):
-            nc.vector.tensor_scalar(
-                out=shifted[:, :, e, :, o],
-                in0=turns_by_parity[:, o],
+        nc.vector.tensor_scalar(out=turns[:, 1], in0=turns[:, 0], scalar1=0.25, scalar2=None, op0=ALU.add)
+        whole = consts.tile([P, 2, N_ANGLES, POS_PER_PART], F32)
+        nc.vector.tensor_scalar(
+            out=whole[:], in0=turns[:], scalar1=ROUND_MAGIC, scalar2=ROUND_MAGIC, op0=ALU.add, op1=ALU.subtract
+        )
+        nc.vector.tensor_tensor(out=turns[:], in0=turns[:], in1=whole[:], op=ALU.subtract)
+
+        transpose_x(0)
+        waves = consts.tile([P, 2, N_ANGLES, POS_PER_PART], F32)
+        nc.scalar.activation(out=waves[:], in_=turns[:], func=ACT.Sin, scale=2.0 * math.pi)
+        nc.scalar.activation(out=warm[:], in_=eps[:], func=ACT.Abs_reciprocal_sqrt)
+        rot = consts.tile([P, POS_PER_PART, 2, PAIRS, 2], F32)
+        for e, o, part, sign in ((0, 0, 1, 1.0), (0, 1, 0, 1.0), (1, 0, 0, -1.0), (1, 1, 1, 1.0)):
+            nc.gpsimd.tensor_scalar(
+                out=rot[:, :, e, :, o],
+                in0=waves[:, part].rearrange("p (i o) t -> p o t i", o=2)[:, o],
                 scalar1=sign,
-                scalar2=quarter,
+                scalar2=0.0,
                 op0=ALU.mult,
                 op1=ALU.add,
             )
-
-        transpose_x(0)
-        gain_acc = psum_front.tile([P, RANK], F32, name="gain_acc", tag="front")
+        gain_acc = psum_q.tile([P, RANK], F32, name="gain_acc", tag="q_nope")
         nc.tensor.matmul(out=gain_acc[:], lhsT=ones[:], rhs=gain_row[:], start=True, stop=True)
-        transpose_x(1)
         quantise_round(-1)
-        whole = consts.tile([P, POS_PER_PART, 2, PAIRS, 2], F32)
-        nc.vector.tensor_scalar(
-            out=whole[:], in0=shifted[:], scalar1=ROUND_MAGIC, scalar2=ROUND_MAGIC, op0=ALU.add, op1=ALU.subtract
-        )
-        nc.vector.tensor_tensor(out=shifted[:], in0=shifted[:], in1=whole[:], op=ALU.subtract)
+        transpose_x(1, nc.vector.tensor_copy)
         gain = consts.tile([P, RANK], F32)
         nc.vector.tensor_copy(out=gain[:], in_=gain_acc[:])
-        first_matmul(0)
-        rot = consts.tile([P, POS_PER_PART, 2, PAIRS, 2], F32)
-        nc.scalar.activation(out=rot[:], in_=shifted[:], func=ACT.Sin, scale=2.0 * math.pi)
+        first_matmul(0, psum_front, "front")
         inverse_norm(0)
         transpose_x(2)
         quantise_round(0)
+        first_matmul(1, psum_q, "q_rope")
+        inverse_norm(1)
 
         def live(g):
             return 0 <= g < N_GROUPS
@@ -306,8 +316,8 @@ def tile_multiheadlatentattention_pa_t_kernel(
         for i in range(1, N_GROUPS + 4):
             if live(i - 1):
                 h = normalise(i - 1)
-            if live(i):
-                first_matmul(i)
+            if live(i) and i > 1:
+                first_matmul(i, psum_front, "front")
                 inverse_norm(i)
             if live(i - 1):
                 transpose_h(i - 1, h)

@@ -44,8 +44,8 @@ def tile_multiheadlatentattention_pa_t_kernel(
 
     with ExitStack() as ctx:
         consts = ctx.enter_context(tc.tile_pool(name="consts", bufs=1))
-        work = ctx.enter_context(tc.tile_pool(name="work", bufs=2))
-        outs = ctx.enter_context(tc.tile_pool(name="outs", bufs=2 * TILES))
+        work = ctx.enter_context(tc.tile_pool(name="work", bufs=3))
+        outs = ctx.enter_context(tc.tile_pool(name="outs", bufs=3))
         results = ctx.enter_context(tc.tile_pool(name="results", bufs=4))
         psum_front = ctx.enter_context(tc.psum_pool(name="psum_front", bufs=4))
         psum_q = ctx.enter_context(tc.psum_pool(name="psum_q", bufs=TILES))
@@ -81,7 +81,8 @@ def tile_multiheadlatentattention_pa_t_kernel(
             b, w = divmod(g, GROUPS_PER_BATCH)
             nc.sync.dma_start(out=x_sb[g][:], in_=x_view[b, :, TILES * w : TILES * (w + 1), :])
 
-        load_x(0)
+        for j in range(TILES):
+            nc.sync.dma_start(out=x_sb[0][:, j, :], in_=x_view[0, :, j, :])
         wqa_codes = consts.tile([P, RANK], U32, align_bytes=64)
         nc.sync.dma_start(
             out=wqa_codes[:].bitcast(I32),
@@ -126,30 +127,36 @@ def tile_multiheadlatentattention_pa_t_kernel(
 
         def transpose_words(src, bank):
             words = src.bitcast(F32)
-            for j in range(TILES):
+            for j in range(src.shape[1]):
                 for u in range(2):
                     nc.tensor.transpose(bank[:, j, u, :], words[:, j, u:WORDS:2], ident[:])
 
-        grouped_of_round = {}
+        grouped_of_round, mx_of_round = {}, {}
 
-        def regroup(bank, rnd, part, copy=nc.scalar.copy):
+        def regroup(bank, rnd, part, tiles, copy):
             if rnd not in grouped_of_round:
                 grouped_of_round[rnd] = work.tile([P, 2, TILES, P, 4], BF16, name="grouped", align_bytes=64)
-            copy(out=grouped_of_round[rnd][:, part].bitcast(F32), in_=bank[:].rearrange("p j u r -> p j r u"))
+            copy(
+                out=grouped_of_round[rnd][:, part, tiles].bitcast(F32),
+                in_=bank[:].rearrange("p j u r -> p j r u"),
+            )
 
-        def quantise(rnd, parts):
-            codes = work.tile([P, 2 * TILES * P], U32, name="codes", align_bytes=64)
-            scales = work.tile([P, 2 * TILES * P], U8, name="scales", align_bytes=64)
-            cols = slice(parts[0] * TILES * P, (parts[-1] + 1) * TILES * P)
+        def quantise(rnd, first, last):
+            if rnd not in mx_of_round:
+                codes = work.tile([P, 2 * TILES * P], U32, name="codes", align_bytes=64)
+                scales = work.tile([P, 2 * TILES * P], U8, name="scales", align_bytes=64)
+                mx_of_round[rnd] = codes, scales
+            codes, scales = mx_of_round[rnd]
+            cols = slice(first * P, last * P)
             nc.vector.quantize_mx(
                 out=codes[:, cols].bitcast(FP8X4),
                 scales=scales[:, cols],
-                in_=grouped_of_round[rnd][:, parts[0] : parts[-1] + 1].rearrange("p a j r t -> p (a j r t)"),
+                in_=grouped_of_round[rnd][:].rearrange("p a j r t -> p (a j r t)")[:, 4 * first * P : 4 * last * P],
             )
-            return codes, scales
 
         def mx_pass(acc, tokens, j, w_codes, w_scales):
-            codes, scales, part = tokens
+            rnd, part = tokens
+            codes, scales = mx_of_round[rnd]
             cols = slice((part * TILES + j) * P, (part * TILES + j + 1) * P)
             nc.tensor.matmul_mx(
                 out=acc[:],
@@ -161,38 +168,43 @@ def tile_multiheadlatentattention_pa_t_kernel(
                 stop=True,
             )
 
-        x_mx, c_acc, sumsq, rstd, h_mx = {}, {}, {}, {}, {}
+        c_acc, sumsq, rstd = {}, {}, {}
         q_rope, terms, result = {}, {}, {}
         held = consts.tile([P, 1], F32)
 
-        def transpose_x(g, copy=nc.scalar.copy):
-            x_t = psum_front.tile([P, TILES, 2, P], F32, name="x_t", tag="front")
-            transpose_words(x_sb[g][:], x_t)
-            regroup(x_t, g - 1, X_PART, copy)
+        def transpose_x(g, copy=nc.scalar.copy, tiles=slice(0, TILES)):
+            x_t = psum_front.tile([P, tiles.stop - tiles.start, 2, P], F32, name="x_t", tag="front")
+            transpose_words(x_sb[g][:, tiles], x_t)
+            regroup(x_t, g - 1, X_PART, tiles, copy)
 
         def quantise_round(rnd):
             parts = [part for part, g in ((X_PART, rnd + 1), (H_PART, rnd - 2)) if 0 <= g < N_GROUPS]
-            codes, scales = quantise(rnd, parts)
-            x_mx[rnd + 1] = (codes, scales, X_PART)
-            h_mx[rnd - 2] = (codes, scales, H_PART)
+            quantise(rnd, TILES * parts[0], TILES * (parts[-1] + 1))
 
-        def first_matmul(g, pool, tag):
+        def first_matmul(g, pool, tag, norm_by_tile=False):
             sumsq[g] = work.tile([P, TILES], F32, name="sumsq")
             c_acc[g] = []
             for j in range(TILES):
                 acc = pool.tile([P, RANK], F32, name="c_acc", tag=tag)
-                mx_pass(acc, x_mx[g], j, wqa_codes[:], wqa_scales[:])
+                mx_pass(acc, (g - 1, X_PART), j, wqa_codes[:], wqa_scales[:])
                 c_acc[g].append(acc)
             for j in range(TILES):
                 squares = work.tile([P, RANK], BF16, name="squares")
                 nc.scalar.activation(
                     out=squares[:], in_=c_acc[g][j][:], func=ACT.Square, accum_out=sumsq[g][:, j : j + 1]
                 )
+                if norm_by_tile:
+                    inverse_norm(g, slice(j, j + 1))
 
-        def inverse_norm(g):
-            rstd[g] = work.tile([P, TILES], F32, name="rstd")
+        def inverse_norm(g, tiles=slice(0, TILES)):
+            if g not in rstd:
+                rstd[g] = work.tile([P, TILES], F32, name="rstd")
             nc.scalar.activation(
-                out=rstd[g][:], in_=sumsq[g][:], func=ACT.Abs_reciprocal_sqrt, scale=1.0 / RANK, bias=eps[:]
+                out=rstd[g][:, tiles],
+                in_=sumsq[g][:, tiles],
+                func=ACT.Abs_reciprocal_sqrt,
+                scale=1.0 / RANK,
+                bias=eps[:],
             )
 
         def normalise(g):
@@ -211,7 +223,7 @@ def tile_multiheadlatentattention_pa_t_kernel(
         def transpose_h(g, h):
             h_t = psum_front.tile([P, TILES, 2, P], F32, name="h_t", tag="front")
             transpose_words(h[:], h_t)
-            regroup(h_t, g + 2, H_PART)
+            regroup(h_t, g + 2, H_PART, slice(0, TILES), nc.scalar.copy)
 
         def second_matmul(g, j):
             if j == 0:
@@ -219,8 +231,8 @@ def tile_multiheadlatentattention_pa_t_kernel(
                 result[g] = results.tile([P, HEADS, TILES, D_NOPE + D_ROPE], F32, name="result")
             q_nope = psum_q.tile([P, HALF_COLS], F32, name="q_nope")
             q_rope[g].append(psum_q.tile([P, HALF_COLS], F32, name="q_rope"))
-            mx_pass(q_nope, h_mx[g], j, wqb_codes[:, 0, :], wqb_scales[:, 0:HALF_COLS])
-            mx_pass(q_rope[g][j], h_mx[g], j, wqb_codes[:, 1, :], wqb_scales[:, HALF_COLS : 2 * HALF_COLS])
+            mx_pass(q_nope, (g + 2, H_PART), j, wqb_codes[:, 0, :], wqb_scales[:, 0:HALF_COLS])
+            mx_pass(q_rope[g][j], (g + 2, H_PART), j, wqb_codes[:, 1, :], wqb_scales[:, HALF_COLS : 2 * HALF_COLS])
             nc.scalar.copy(
                 out=result[g][:, :, j, 0:D_NOPE], in_=q_nope[:].rearrange("p (h d) -> p h d", d=D_NOPE)
             )
@@ -229,10 +241,9 @@ def tile_multiheadlatentattention_pa_t_kernel(
             t = TILES * (g % GROUPS_PER_BATCH) + j
             shape = [P, 2, HEADS * 2, PAIRS, 2]
             if j == 0:
-                terms[g] = []
-            terms[g].append(outs.tile([P, 2, HALF_COLS], F32, name="terms"))
+                terms[g] = outs.tile([P, TILES, 2, HALF_COLS], F32, name="terms")
             nc.vector.tensor_tensor(
-                out=terms[g][j][:].rearrange("p e (hr i o) -> p e hr i o", i=PAIRS, o=2),
+                out=terms[g][:, j].rearrange("p e (hr i o) -> p e hr i o", i=PAIRS, o=2),
                 in0=q_rope[g][j][:]
                 .rearrange("p (hr i e) -> p e hr i", e=2, i=PAIRS)
                 .unsqueeze(4)
@@ -241,20 +252,20 @@ def tile_multiheadlatentattention_pa_t_kernel(
                 op=ALU.mult,
             )
 
-        def hold_gpsimd_for(tokens):
-            codes, scales, part = tokens
+        def hold_gpsimd_for(rnd, part):
+            codes, scales = mx_of_round[rnd]
             first = part * TILES * P
             nc.gpsimd.tensor_copy(out=held[:], in_=codes[:, first : first + 1].bitcast(F32))
 
         def add_terms_and_store(engine, g, j):
             engine.tensor_tensor(
                 out=result[g][:, :, j, D_NOPE:],
-                in0=terms[g][j][:, 0, :].rearrange("p (h d) -> p h d", d=D_ROPE),
-                in1=terms[g][j][:, 1, :].rearrange("p (h d) -> p h d", d=D_ROPE),
+                in0=terms[g][:, j, 0, :].rearrange("p (h d) -> p h d", d=D_ROPE),
+                in1=terms[g][:, j, 1, :].rearrange("p (h d) -> p h d", d=D_ROPE),
                 op=ALU.add,
             )
             b, w = divmod(g, GROUPS_PER_BATCH)
-            if g == N_GROUPS - 1:
+            if g >= N_GROUPS - 2:
                 nc.sync.dma_start(out=out_view[b, :, :, TILES * w + j, :], in_=result[g][:, :, j, :])
             elif j == TILES - 1:
                 nc.sync.dma_start(out=out_view[b, :, :, TILES * w : TILES * (w + 1), :], in_=result[g][:])
@@ -283,7 +294,8 @@ def tile_multiheadlatentattention_pa_t_kernel(
         )
         nc.vector.tensor_tensor(out=turns[:], in0=turns[:], in1=whole[:], op=ALU.subtract)
 
-        transpose_x(0)
+        for j in range(TILES):
+            transpose_x(0, tiles=slice(j, j + 1))
         waves = consts.tile([P, 2, N_ANGLES, POS_PER_PART], F32)
         nc.scalar.activation(out=waves[:], in_=turns[:], func=ACT.Sin, scale=2.0 * math.pi)
         nc.scalar.activation(out=warm[:], in_=eps[:], func=ACT.Abs_reciprocal_sqrt)
@@ -299,12 +311,12 @@ def tile_multiheadlatentattention_pa_t_kernel(
             )
         gain_acc = psum_q.tile([P, RANK], F32, name="gain_acc", tag="q_nope")
         nc.tensor.matmul(out=gain_acc[:], lhsT=ones[:], rhs=gain_row[:], start=True, stop=True)
-        quantise_round(-1)
+        for j in range(TILES):
+            quantise(-1, j, j + 1)
         transpose_x(1, nc.vector.tensor_copy)
         gain = consts.tile([P, RANK], F32)
         nc.vector.tensor_copy(out=gain[:], in_=gain_acc[:])
-        first_matmul(0, psum_front, "front")
-        inverse_norm(0)
+        first_matmul(0, psum_front, "front", norm_by_tile=True)
         transpose_x(2)
         quantise_round(0)
         first_matmul(1, psum_q, "q_rope")
@@ -327,9 +339,9 @@ def tile_multiheadlatentattention_pa_t_kernel(
                 quantise_round(i)
             if live(i - 4):
                 if live(i + 1):
-                    hold_gpsimd_for(x_mx[i + 1])
+                    hold_gpsimd_for(i, X_PART)
                 elif live(i - 2):
-                    hold_gpsimd_for(h_mx[i - 2])
+                    hold_gpsimd_for(i, H_PART)
                 add_terms_and_store(nc.gpsimd if live(i - 3) else nc.vector, i - 4, TILES - 1)
             for j in range(TILES):
                 if live(i - 3):

@@ -53,9 +53,13 @@ def tile_multiheadlatentattention_pa_t_kernel(
 
         wqa_scales = consts.tile([P, RANK], U8, align_bytes=64)
         wqb_scales = consts.tile([P, 2 * HALF_COLS], U8, align_bytes=64)
+        gain_row = consts.tile([P, RANK], BF16)
+        nc.vector.memset(gain_row[:], 0.0)
         nc.vector.memset(wqa_scales[:].bitcast(I32), 0)
         eps = consts.tile([P, 1], F32)
         nc.vector.memset(eps[:], EPS)
+        ones = consts.tile([P, P], BF16)
+        nc.vector.memset(ones[:], 1.0)
         pos = consts.tile([P, POS_PER_PART], F32)
         nc.gpsimd.iota(
             pos[:],
@@ -66,10 +70,6 @@ def tile_multiheadlatentattention_pa_t_kernel(
         )
         ident = consts.tile([P, P], F32)
         masks.make_identity(nc, ident[:])
-        gain_row = consts.tile([P, RANK], BF16)
-        nc.gpsimd.memset(gain_row[:], 0.0)
-        ones = consts.tile([P, P], BF16)
-        nc.gpsimd.memset(ones[:], 1.0)
         nc.gpsimd.memset(wqb_scales[:].bitcast(I32), 0)
 
         warm = consts.tile([P, 1], F32)
@@ -81,8 +81,8 @@ def tile_multiheadlatentattention_pa_t_kernel(
             b, w = divmod(g, GROUPS_PER_BATCH)
             nc.sync.dma_start(out=x_sb[g][:], in_=x_view[b, :, TILES * w : TILES * (w + 1), :])
 
-        for j in range(TILES):
-            nc.sync.dma_start(out=x_sb[0][:, j, :], in_=x_view[0, :, j, :])
+        load_x(0)
+        nc.sync.dma_start(out=gain_row[0:1, :], in_=q_a_norm_w.unsqueeze(0))
         wqa_codes = consts.tile([P, RANK], U32, align_bytes=64)
         nc.sync.dma_start(
             out=wqa_codes[:].bitcast(I32),
@@ -93,7 +93,6 @@ def tile_multiheadlatentattention_pa_t_kernel(
                 out=wqa_scales[32 * quad : 32 * quad + 4, :].bitcast(I32),
                 in_=Wqa_scales[0, 4 * quad : 4 * quad + 4, :].bitcast(I32),
             )
-        nc.sync.dma_start(out=gain_row[0:1, :], in_=q_a_norm_w.unsqueeze(0))
         load_x(1)
         load_x(2)
         load_x(3)

@@ -52,7 +52,7 @@ def tile_multiheadlatentattention_pa_t_kernel(
         ctx.enter_context(tc.manual_schedule())
 
         wqa_scales = consts.tile([P, RANK], U8, align_bytes=64)
-        wqb_scales = consts.tile([P, 2 * HALF_COLS], U8, align_bytes=64)
+        wqb_scale_rows = consts.tile([P, 2 * HALF_COLS], U8, align_bytes=64)
         gain_row = consts.tile([P, RANK], BF16)
         nc.vector.memset(gain_row[:], 0.0)
         nc.vector.memset(wqa_scales[:].bitcast(I32), 0)
@@ -60,6 +60,7 @@ def tile_multiheadlatentattention_pa_t_kernel(
         nc.vector.memset(eps[:], EPS)
         ones = consts.tile([P, P], BF16)
         nc.vector.memset(ones[:], 1.0)
+        nc.vector.memset(wqb_scale_rows[:].bitcast(I32), 0)
         pos = consts.tile([P, POS_PER_PART], F32)
         nc.gpsimd.iota(
             pos[:],
@@ -70,7 +71,6 @@ def tile_multiheadlatentattention_pa_t_kernel(
         )
         ident = consts.tile([P, P], F32)
         masks.make_identity(nc, ident[:])
-        nc.gpsimd.memset(wqb_scales[:].bitcast(I32), 0)
 
         warm = consts.tile([P, 1], F32)
         nc.scalar.activation(out=warm[:], in_=eps[:], func=ACT.Sin)
@@ -95,33 +95,23 @@ def tile_multiheadlatentattention_pa_t_kernel(
             )
         load_x(1)
         load_x(2)
-        load_x(3)
+        for quad in range(4):
+            nc.sync.dma_start(
+                out=wqb_scale_rows[32 * quad : 32 * quad + 4, :].bitcast(I32),
+                in_=Wqb_scales[0, 4 * quad : 4 * quad + 4, :].bitcast(I32),
+            )
         wqb_codes = consts.tile([P, 2, HALF_COLS], U32, align_bytes=64)
         wqb_words_src = (
             Wqb_words.rearrange("g p n t -> (g p) (n t)")
             .bitcast(I32)
             .rearrange("p (h half d) -> p half h d", half=2, d=D_NOPE)
         )
-        wqb_scales_src = Wqb_scales[0].bitcast(I32).rearrange(
-            "q (h half d) -> q half h d", half=2, d=D_NOPE // 4
-        )
-        wqb_scales_dst = wqb_scales[:].bitcast(I32).rearrange(
-            "p (half h d) -> p half h d", half=2, d=D_NOPE // 4
-        )
         for half in range(2):
             nc.sync.dma_start(
                 out=wqb_codes[:, half, :].bitcast(I32).rearrange("p (h d) -> p h d", d=D_NOPE),
                 in_=wqb_words_src[:, half],
             )
-        load_x(4)
-        load_x(5)
-        for half in range(2):
-            for quad in range(4):
-                nc.sync.dma_start(
-                    out=wqb_scales_dst[32 * quad : 32 * quad + 4, half],
-                    in_=wqb_scales_src[4 * quad : 4 * quad + 4, half],
-                )
-        for g in range(6, N_GROUPS):
+        for g in range(3, N_GROUPS):
             load_x(g)
 
         def transpose_words(src, bank):
@@ -308,6 +298,11 @@ def tile_multiheadlatentattention_pa_t_kernel(
                 op0=ALU.mult,
                 op1=ALU.add,
             )
+        wqb_scales = consts.tile([P, 2 * HALF_COLS], U8, align_bytes=64)
+        nc.gpsimd.tensor_copy(
+            out=wqb_scales[:].bitcast(I32).rearrange("p (half h d) -> p half h d", half=2, d=D_NOPE // 4),
+            in_=wqb_scale_rows[:].bitcast(I32).rearrange("p (h half d) -> p half h d", half=2, d=D_NOPE // 4),
+        )
         gain_acc = psum_q.tile([P, RANK], F32, name="gain_acc", tag="q_nope")
         nc.tensor.matmul(out=gain_acc[:], lhsT=ones[:], rhs=gain_row[:], start=True, stop=True)
         for j in range(TILES):

@@ -53,14 +53,33 @@ def tile_multiheadlatentattention_pa_t_kernel(
 
         wqa_scales = consts.tile([P, RANK], U8, align_bytes=64)
         wqb_scale_rows = consts.tile([P, 2 * HALF_COLS], U8, align_bytes=64)
+        one = consts.tile([P, 1], F32)
+        nc.vector.memset(one[:], 1.0)
+        ones = consts.tile([P, P], BF16)
+        nc.vector.memset(ones[:], 1.0)
         gain_row = consts.tile([P, RANK], BF16)
         nc.vector.memset(gain_row[:], 0.0)
         nc.vector.memset(wqa_scales[:].bitcast(I32), 0)
         eps = consts.tile([P, 1], F32)
         nc.vector.memset(eps[:], EPS)
-        ones = consts.tile([P, P], BF16)
-        nc.vector.memset(ones[:], 1.0)
+        turns_per_pos = consts.tile([P, N_ANGLES], F32)
+        for n in range(8):
+            nc.vector.tensor_scalar(
+                out=turns_per_pos[:, n : n + 1],
+                in0=one[:],
+                scalar1=THETA ** (-n / N_ANGLES) / (2.0 * math.pi),
+                scalar2=None,
+                op0=ALU.mult,
+            )
         nc.vector.memset(wqb_scale_rows[:].bitcast(I32), 0)
+        for n in (8, 16):
+            nc.vector.tensor_scalar(
+                out=turns_per_pos[:, n : 2 * n],
+                in0=turns_per_pos[:, 0:n],
+                scalar1=THETA ** (-n / N_ANGLES),
+                scalar2=None,
+                op0=ALU.mult,
+            )
         pos = consts.tile([P, POS_PER_PART], F32)
         nc.gpsimd.iota(
             pos[:],
@@ -226,14 +245,15 @@ def tile_multiheadlatentattention_pa_t_kernel(
                 out=result[g][:, :, j, 0:D_NOPE], in_=q_nope[:].rearrange("p (h d) -> p h d", d=D_NOPE)
             )
 
-        def rotate_terms(g, j):
+        def rotate_terms(g, j, heads=slice(0, HEADS)):
             t = TILES * (g % GROUPS_PER_BATCH) + j
-            shape = [P, 2, HEADS * 2, PAIRS, 2]
-            if j == 0:
+            cols = slice(heads.start * D_ROPE, heads.stop * D_ROPE)
+            shape = [P, 2, 2 * (heads.stop - heads.start), PAIRS, 2]
+            if g not in terms:
                 terms[g] = outs.tile([P, TILES, 2, HALF_COLS], F32, name="terms")
             nc.vector.tensor_tensor(
-                out=terms[g][:, j].rearrange("p e (hr i o) -> p e hr i o", i=PAIRS, o=2),
-                in0=q_rope[g][j][:]
+                out=terms[g][:, j, :, cols].rearrange("p e (hr i o) -> p e hr i o", i=PAIRS, o=2),
+                in0=q_rope[g][j][:, cols]
                 .rearrange("p (hr i e) -> p e hr i", e=2, i=PAIRS)
                 .unsqueeze(4)
                 .to_broadcast(shape),
@@ -246,43 +266,58 @@ def tile_multiheadlatentattention_pa_t_kernel(
             first = part * TILES * P
             nc.gpsimd.tensor_copy(out=held[:], in_=codes[:, first : first + 1].bitcast(F32))
 
-        def add_terms_and_store(engine, g, j):
+        def add_terms(engine, g, j, heads=slice(0, HEADS)):
+            cols = slice(heads.start * D_ROPE, heads.stop * D_ROPE)
             engine.tensor_tensor(
-                out=result[g][:, :, j, D_NOPE:],
-                in0=terms[g][:, j, 0, :].rearrange("p (h d) -> p h d", d=D_ROPE),
-                in1=terms[g][:, j, 1, :].rearrange("p (h d) -> p h d", d=D_ROPE),
+                out=result[g][:, heads, j, D_NOPE:],
+                in0=terms[g][:, j, 0, cols].rearrange("p (h d) -> p h d", d=D_ROPE),
+                in1=terms[g][:, j, 1, cols].rearrange("p (h d) -> p h d", d=D_ROPE),
                 op=ALU.add,
             )
+
+        def store(g, tiles, heads=slice(0, HEADS)):
             b, w = divmod(g, GROUPS_PER_BATCH)
+            rows = slice(TILES * w + tiles.start, TILES * w + tiles.stop)
+            nc.sync.dma_start(out=out_view[b, :, heads, rows, :], in_=result[g][:, heads, tiles, :])
+
+        def store_after(g, j):
             if g >= N_GROUPS - 2:
-                nc.sync.dma_start(out=out_view[b, :, :, TILES * w + j, :], in_=result[g][:, :, j, :])
+                store(g, slice(j, j + 1))
             elif j == TILES - 1:
-                nc.sync.dma_start(out=out_view[b, :, :, TILES * w : TILES * (w + 1), :], in_=result[g][:])
+                store(g, slice(0, TILES))
 
         turns = consts.tile([P, 2, N_ANGLES, POS_PER_PART], F32)
-        for n in range(4):
-            nc.vector.tensor_scalar(
-                out=turns[:, 0, n, :],
-                in0=pos[:],
-                scalar1=THETA ** (-n / N_ANGLES) / (2.0 * math.pi),
-                scalar2=None,
-                op0=ALU.mult,
-            )
-        for n in (4, 8, 16):
-            nc.vector.tensor_scalar(
-                out=turns[:, 0, n : 2 * n, :],
-                in0=turns[:, 0, 0:n, :],
-                scalar1=THETA ** (-n / N_ANGLES),
-                scalar2=None,
-                op0=ALU.mult,
-            )
-        nc.vector.tensor_scalar(out=turns[:, 1], in0=turns[:, 0], scalar1=0.25, scalar2=None, op0=ALU.add)
         whole = consts.tile([P, 2, N_ANGLES, POS_PER_PART], F32)
-        nc.vector.tensor_scalar(
-            out=whole[:], in0=turns[:], scalar1=ROUND_MAGIC, scalar2=ROUND_MAGIC, op0=ALU.add, op1=ALU.subtract
-        )
-        nc.vector.tensor_tensor(out=turns[:], in0=turns[:], in1=whole[:], op=ALU.subtract)
+        angles = [P, N_ANGLES, POS_PER_PART]
 
+        def nearest_integer(part):
+            nc.vector.tensor_scalar(
+                out=whole[:, part],
+                in0=turns[:, part],
+                scalar1=ROUND_MAGIC,
+                scalar2=ROUND_MAGIC,
+                op0=ALU.add,
+                op1=ALU.subtract,
+            )
+
+        def take_off_integer(part):
+            nc.vector.tensor_tensor(out=turns[:, part], in0=turns[:, part], in1=whole[:, part], op=ALU.subtract)
+
+        nc.vector.tensor_tensor(
+            out=turns[:, 0],
+            in0=turns_per_pos[:].unsqueeze(2).to_broadcast(angles),
+            in1=pos[:].unsqueeze(1).to_broadcast(angles),
+            op=ALU.mult,
+        )
+        nc.vector.tensor_scalar(out=turns[:, 1], in0=turns[:, 0], scalar1=0.25, scalar2=None, op0=ALU.add)
+        nearest_integer(0)
+        nearest_integer(1)
+        take_off_integer(0)
+        take_off_integer(1)
+
+        warm_acc = psum_q.tile([P, P], F32, name="warm_acc", tag="q_rope")
+        for repeat in range(16):
+            nc.tensor.matmul(out=warm_acc[:], lhsT=ones[:], rhs=ones[:], start=True, stop=True)
         for j in range(TILES):
             transpose_x(0, tiles=slice(j, j + 1))
         waves = consts.tile([P, 2, N_ANGLES, POS_PER_PART], F32)
@@ -319,7 +354,7 @@ def tile_multiheadlatentattention_pa_t_kernel(
         def live(g):
             return 0 <= g < N_GROUPS
 
-        for i in range(1, N_GROUPS + 4):
+        for i in range(1, N_GROUPS + 3):
             if live(i - 1):
                 h = normalise(i - 1)
             if live(i) and i > 1:
@@ -331,16 +366,29 @@ def tile_multiheadlatentattention_pa_t_kernel(
                 transpose_x(i + 2)
             if live(i + 1) or live(i - 2):
                 quantise_round(i)
-            if live(i - 4):
+            if live(i - 4) and live(i - 3):
                 if live(i + 1):
                     hold_gpsimd_for(i, X_PART)
                 elif live(i - 2):
                     hold_gpsimd_for(i, H_PART)
-                add_terms_and_store(nc.gpsimd if live(i - 3) else nc.vector, i - 4, TILES - 1)
+                add_terms(nc.gpsimd, i - 4, TILES - 1)
+                store_after(i - 4, TILES - 1)
             for j in range(TILES):
-                if live(i - 3):
+                if live(i - 3) and live(i - 2):
                     rotate_terms(i - 3, j)
                     if j < TILES - 1:
-                        add_terms_and_store(nc.gpsimd, i - 3, j)
+                        add_terms(nc.gpsimd, i - 3, j)
+                        store_after(i - 3, j)
                 if live(i - 2):
                     second_matmul(i - 2, j)
+
+        last, last_tile = N_GROUPS - 1, slice(TILES - 1, TILES)
+        halves = slice(0, HEADS // 2), slice(HEADS // 2, HEADS)
+        rotate_terms(last, 0)
+        rotate_terms(last, 1, halves[0])
+        add_terms(nc.vector, last, 0)
+        store_after(last, 0)
+        rotate_terms(last, 1, halves[1])
+        for heads in halves:
+            add_terms(nc.vector, last, 1, heads)
+            store(last, last_tile, heads)

@@ -46,7 +46,7 @@ def tile_multiheadlatentattention_pa_t_kernel(
         consts = ctx.enter_context(tc.tile_pool(name="consts", bufs=1))
         work = ctx.enter_context(tc.tile_pool(name="work", bufs=3))
         outs = ctx.enter_context(tc.tile_pool(name="outs", bufs=3))
-        results = ctx.enter_context(tc.tile_pool(name="results", bufs=4))
+        results = ctx.enter_context(tc.tile_pool(name="results", bufs=14))
         psum_front = ctx.enter_context(tc.psum_pool(name="psum_front", bufs=4))
         psum_q = ctx.enter_context(tc.psum_pool(name="psum_q", bufs=TILES))
         ctx.enter_context(tc.manual_schedule())
@@ -281,7 +281,7 @@ def tile_multiheadlatentattention_pa_t_kernel(
             nc.sync.dma_start(out=out_view[b, :, heads, rows, :], in_=result[g][:, heads, tiles, :])
 
         def store_after(g, j):
-            if g >= N_GROUPS - 2:
+            if g == N_GROUPS - 1:
                 store(g, slice(j, j + 1))
             elif j == TILES - 1:
                 store(g, slice(0, TILES))

@@ -46,7 +46,7 @@ def tile_multiheadlatentattention_pa_t_kernel(
         consts = ctx.enter_context(tc.tile_pool(name="consts", bufs=1))
         work = ctx.enter_context(tc.tile_pool(name="work", bufs=3))
         outs = ctx.enter_context(tc.tile_pool(name="outs", bufs=3))
-        results = ctx.enter_context(tc.tile_pool(name="results", bufs=14))
+        results = ctx.enter_context(tc.tile_pool(name="results", bufs=16))
         psum_front = ctx.enter_context(tc.psum_pool(name="psum_front", bufs=4))
         psum_q = ctx.enter_context(tc.psum_pool(name="psum_q", bufs=TILES))
         ctx.enter_context(tc.manual_schedule())
@@ -275,16 +275,11 @@ def tile_multiheadlatentattention_pa_t_kernel(
                 op=ALU.add,
             )
 
-        def store(g, tiles, heads=slice(0, HEADS)):
+        def store(g, heads=slice(0, HEADS)):
             b, w = divmod(g, GROUPS_PER_BATCH)
-            rows = slice(TILES * w + tiles.start, TILES * w + tiles.stop)
-            nc.sync.dma_start(out=out_view[b, :, heads, rows, :], in_=result[g][:, heads, tiles, :])
-
-        def store_after(g, j):
-            if g == N_GROUPS - 1:
-                store(g, slice(j, j + 1))
-            elif j == TILES - 1:
-                store(g, slice(0, TILES))
+            nc.sync.dma_start(
+                out=out_view[b, :, heads, TILES * w : TILES * (w + 1), :], in_=result[g][:, heads]
+            )
 
         turns = consts.tile([P, 2, N_ANGLES, POS_PER_PART], F32)
         whole = consts.tile([P, 2, N_ANGLES, POS_PER_PART], F32)
@@ -372,23 +367,22 @@ def tile_multiheadlatentattention_pa_t_kernel(
                 elif live(i - 2):
                     hold_gpsimd_for(i, H_PART)
                 add_terms(nc.gpsimd, i - 4, TILES - 1)
-                store_after(i - 4, TILES - 1)
+                store(i - 4)
             for j in range(TILES):
                 if live(i - 3) and live(i - 2):
                     rotate_terms(i - 3, j)
                     if j < TILES - 1:
                         add_terms(nc.gpsimd, i - 3, j)
-                        store_after(i - 3, j)
                 if live(i - 2):
                     second_matmul(i - 2, j)
 
-        last, last_tile = N_GROUPS - 1, slice(TILES - 1, TILES)
-        halves = slice(0, HEADS // 2), slice(HEADS // 2, HEADS)
+        last = N_GROUPS - 1
+        first_heads, last_heads = slice(0, HEADS // 2), slice(HEADS // 2, HEADS)
         rotate_terms(last, 0)
-        rotate_terms(last, 1, halves[0])
+        rotate_terms(last, 1, first_heads)
         add_terms(nc.vector, last, 0)
-        store_after(last, 0)
-        rotate_terms(last, 1, halves[1])
-        for heads in halves:
-            add_terms(nc.vector, last, 1, heads)
-            store(last, last_tile, heads)
+        add_terms(nc.vector, last, 1, first_heads)
+        store(last, first_heads)
+        rotate_terms(last, 1, last_heads)
+        add_terms(nc.vector, last, 1, last_heads)
+        store(last, last_heads)

import math
from contextlib import ExitStack

import concourse.masks as masks
import concourse.mybir as mybir

F32 = mybir.dt.float32
BF16 = mybir.dt.bfloat16
I32 = mybir.dt.int32
U32 = mybir.dt.uint32
U8 = mybir.dt.uint8
FP8X4 = mybir.dt.float8_e4m3fn_x4
ALU = mybir.AluOpType
ACT = mybir.ActivationFunctionType

P = 128
BATCH, SEQ, D_MODEL = 4, 1024, 512
HEADS, D_NOPE, D_ROPE = 8, 64, 64
RANK = 512
HALF_COLS = HEADS * D_NOPE
THETA = 10000.0
EPS = 1e-6

POS_PER_PART = SEQ // P
TILES = 2
GROUPS_PER_BATCH = POS_PER_PART // TILES
N_GROUPS = BATCH * GROUPS_PER_BATCH
WORDS = D_MODEL // 2

N_ANGLES = D_ROPE // 2
X_PART, H_PART = 0, 1
PAIRS = N_ANGLES // 2
ROUND_MAGIC = 1.5 * 2.0**23

FLOPS = 2 * BATCH * SEQ * (D_MODEL * RANK + RANK * 2 * HALF_COLS)


def tile_multiheadlatentattention_pa_t_kernel(
    tc, x, Wqa_words, Wqa_scales, q_a_norm_w, Wqb_words, Wqb_scales, out
):
    nc = tc.nc
    x_view = x.rearrange("b (p t) k -> b p t k", t=POS_PER_PART)
    out_view = out.rearrange("b h (p t) d -> b p h t d", t=POS_PER_PART)

    with ExitStack() as ctx:
        consts = ctx.enter_context(tc.tile_pool(name="consts", bufs=1))
        work = ctx.enter_context(tc.tile_pool(name="work", bufs=3))
        outs = ctx.enter_context(tc.tile_pool(name="outs", bufs=3))
        results = ctx.enter_context(tc.tile_pool(name="results", bufs=16))
        psum_front = ctx.enter_context(tc.psum_pool(name="psum_front", bufs=4))
        psum_q = ctx.enter_context(tc.psum_pool(name="psum_q", bufs=TILES))
        ctx.enter_context(tc.manual_schedule())

        wqa_scales = consts.tile([P, RANK], U8, align_bytes=64)
        wqb_scale_rows = consts.tile([P, 2 * HALF_COLS], U8, align_bytes=64)
        one = consts.tile([P, 1], F32)
        nc.vector.memset(one[:], 1.0)
        ones = consts.tile([P, P], BF16)
        nc.vector.memset(ones[:], 1.0)
        gain_row = consts.tile([P, RANK], BF16)
        nc.vector.memset(gain_row[:], 0.0)
        nc.vector.memset(wqa_scales[:].bitcast(I32), 0)
        eps = consts.tile([P, 1], F32)
        nc.vector.memset(eps[:], EPS)
        turns_per_pos = consts.tile([P, N_ANGLES], F32)
        for n in range(8):
            nc.vector.tensor_scalar(
                out=turns_per_pos[:, n : n + 1],
                in0=one[:],
                scalar1=THETA ** (-n / N_ANGLES) / (2.0 * math.pi),
                scalar2=None,
                op0=ALU.mult,
            )
        nc.vector.memset(wqb_scale_rows[:].bitcast(I32), 0)
        for n in (8, 16):
            nc.vector.tensor_scalar(
                out=turns_per_pos[:, n : 2 * n],
                in0=turns_per_pos[:, 0:n],
                scalar1=THETA ** (-n / N_ANGLES),
                scalar2=None,
                op0=ALU.mult,
            )
        pos = consts.tile([P, POS_PER_PART], F32)
        nc.gpsimd.iota(
            pos[:],
            pattern=[[1, POS_PER_PART]],
            base=0,
            channel_multiplier=POS_PER_PART,
            allow_small_or_imprecise_dtypes=True,
        )
        ident = consts.tile([P, P], F32)
        masks.make_identity(nc, ident[:])

        warm = consts.tile([P, 1], F32)
        nc.scalar.activation(out=warm[:], in_=eps[:], func=ACT.Sin)

        x_sb = [consts.tile([P, TILES, D_MODEL], BF16, name="x%d" % g) for g in range(N_GROUPS)]

        def load_x(g):
            b, w = divmod(g, GROUPS_PER_BATCH)
            nc.sync.dma_start(out=x_sb[g][:], in_=x_view[b, :, TILES * w : TILES * (w + 1), :])

        load_x(0)
        nc.sync.dma_start(out=gain_row[0:1, :], in_=q_a_norm_w.unsqueeze(0))
        wqa_codes = consts.tile([P, RANK], U32, align_bytes=64)
        nc.sync.dma_start(
            out=wqa_codes[:].bitcast(I32),
            in_=Wqa_words.rearrange("g p n t -> (g p) (n t)").bitcast(I32),
        )
        for quad in range(4):
            nc.sync.dma_start(
                out=wqa_scales[32 * quad : 32 * quad + 4, :].bitcast(I32),
                in_=Wqa_scales[0, 4 * quad : 4 * quad + 4, :].bitcast(I32),
            )
        load_x(1)
        load_x(2)
        for quad in range(4):
            nc.sync.dma_start(
                out=wqb_scale_rows[32 * quad : 32 * quad + 4, :].bitcast(I32),
                in_=Wqb_scales[0, 4 * quad : 4 * quad + 4, :].bitcast(I32),
            )
        wqb_codes = consts.tile([P, 2, HALF_COLS], U32, align_bytes=64)
        wqb_words_src = (
            Wqb_words.rearrange("g p n t -> (g p) (n t)")
            .bitcast(I32)
            .rearrange("p (h half d) -> p half h d", half=2, d=D_NOPE)
        )
        for half in range(2):
            nc.sync.dma_start(
                out=wqb_codes[:, half, :].bitcast(I32).rearrange("p (h d) -> p h d", d=D_NOPE),
                in_=wqb_words_src[:, half],
            )
        for g in range(3, N_GROUPS):
            load_x(g)

        def transpose_words(src, bank):
            words = src.bitcast(F32)
            for j in range(src.shape[1]):
                for u in range(2):
                    nc.tensor.transpose(bank[:, j, u, :], words[:, j, u:WORDS:2], ident[:])

        grouped_of_round, mx_of_round = {}, {}

        def regroup(bank, rnd, part, tiles, copy):
            if rnd not in grouped_of_round:
                grouped_of_round[rnd] = work.tile([P, 2, TILES, P, 4], BF16, name="grouped", align_bytes=64)
            copy(
                out=grouped_of_round[rnd][:, part, tiles].bitcast(F32),
                in_=bank[:].rearrange("p j u r -> p j r u"),
            )

        def quantise(rnd, first, last):
            if rnd not in mx_of_round:
                codes = work.tile([P, 2 * TILES * P], U32, name="codes", align_bytes=64)
                scales = work.tile([P, 2 * TILES * P], U8, name="scales", align_bytes=64)
                mx_of_round[rnd] = codes, scales
            codes, scales = mx_of_round[rnd]
            cols = slice(first * P, last * P)
            nc.vector.quantize_mx(
                out=codes[:, cols].bitcast(FP8X4),
                scales=scales[:, cols],
                in_=grouped_of_round[rnd][:].rearrange("p a j r t -> p (a j r t)")[:, 4 * first * P : 4 * last * P],
            )

        def mx_pass(acc, tokens, j, w_codes, w_scales):
            rnd, part = tokens
            codes, scales = mx_of_round[rnd]
            cols = slice((part * TILES + j) * P, (part * TILES + j + 1) * P)
            nc.tensor.matmul_mx(
                out=acc[:],
                lhsT=codes[:, cols].bitcast(FP8X4),
                lhsT_scale=scales[:, cols],
                rhs=w_codes.bitcast(FP8X4),
                rhs_scale=w_scales,
                start=True,
                stop=True,
            )

        c_acc, sumsq, rstd = {}, {}, {}
        q_rope, terms, result = {}, {}, {}
        held = consts.tile([P, 1], F32)

        def transpose_x(g, copy=nc.scalar.copy, tiles=slice(0, TILES)):
            x_t = psum_front.tile([P, tiles.stop - tiles.start, 2, P], F32, name="x_t", tag="front")
            transpose_words(x_sb[g][:, tiles], x_t)
            regroup(x_t, g - 1, X_PART, tiles, copy)

        def quantise_round(rnd):
            parts = [part for part, g in ((X_PART, rnd + 1), (H_PART, rnd - 2)) if 0 <= g < N_GROUPS]
            quantise(rnd, TILES * parts[0], TILES * (parts[-1] + 1))

        def first_matmul(g, pool, tag, norm_by_tile=False):
            sumsq[g] = work.tile([P, TILES], F32, name="sumsq")
            c_acc[g] = []
            for j in range(TILES):
                acc = pool.tile([P, RANK], F32, name="c_acc", tag=tag)
                mx_pass(acc, (g - 1, X_PART), j, wqa_codes[:], wqa_scales[:])
                c_acc[g].append(acc)
            for j in range(TILES):
                squares = work.tile([P, RANK], BF16, name="squares")
                nc.scalar.activation(
                    out=squares[:], in_=c_acc[g][j][:], func=ACT.Square, accum_out=sumsq[g][:, j : j + 1]
                )
                if norm_by_tile:
                    inverse_norm(g, slice(j, j + 1))

        def inverse_norm(g, tiles=slice(0, TILES)):
            if g not in rstd:
                rstd[g] = work.tile([P, TILES], F32, name="rstd")
            nc.scalar.activation(
                out=rstd[g][:, tiles],
                in_=sumsq[g][:, tiles],
                func=ACT.Abs_reciprocal_sqrt,
                scale=1.0 / RANK,
                bias=eps[:],
            )

        def normalise(g):
            h = work.tile([P, TILES, RANK], BF16, name="h")
            for j in range(TILES):
                nc.vector.scalar_tensor_tensor(
                    out=h[:, j, :],
                    in0=c_acc[g][j][:],
                    scalar=rstd[g][:, j : j + 1],
                    in1=gain[:],
                    op0=ALU.mult,
                    op1=ALU.mult,
                )
            return h

        def transpose_h(g, h):
            h_t = psum_front.tile([P, TILES, 2, P], F32, name="h_t", tag="front")
            transpose_words(h[:], h_t)
            regroup(h_t, g + 2, H_PART, slice(0, TILES), nc.scalar.copy)

        def second_matmul(g, j):
            if j == 0:
                q_rope[g] = []
                result[g] = results.tile([P, HEADS, TILES, D_NOPE + D_ROPE], F32, name="result")
            q_nope = psum_q.tile([P, HALF_COLS], F32, name="q_nope")
            q_rope[g].append(psum_q.tile([P, HALF_COLS], F32, name="q_rope"))
            mx_pass(q_nope, (g + 2, H_PART), j, wqb_codes[:, 0, :], wqb_scales[:, 0:HALF_COLS])
            mx_pass(q_rope[g][j], (g + 2, H_PART), j, wqb_codes[:, 1, :], wqb_scales[:, HALF_COLS : 2 * HALF_COLS])
            nc.scalar.copy(
                out=result[g][:, :, j, 0:D_NOPE], in_=q_nope[:].rearrange("p (h d) -> p h d", d=D_NOPE)
            )

        def rotate_terms(g, j, heads=slice(0, HEADS)):
            t = TILES * (g % GROUPS_PER_BATCH) + j
            cols = slice(heads.start * D_ROPE, heads.stop * D_ROPE)
            shape = [P, 2, 2 * (heads.stop - heads.start), PAIRS, 2]
            if g not in terms:
                terms[g] = outs.tile([P, TILES, 2, HALF_COLS], F32, name="terms")
            nc.vector.tensor_tensor(
                out=terms[g][:, j, :, cols].rearrange("p e (hr i o) -> p e hr i o", i=PAIRS, o=2),
                in0=q_rope[g][j][:, cols]
                .rearrange("p (hr i e) -> p e hr i", e=2, i=PAIRS)
                .unsqueeze(4)
                .to_broadcast(shape),
                in1=rot[:, t].unsqueeze(2).to_broadcast(shape),
                op=ALU.mult,
            )

        def hold_gpsimd_for(rnd, part):
            codes, scales = mx_of_round[rnd]
            first = part * TILES * P
            nc.gpsimd.tensor_copy(out=held[:], in_=codes[:, first : first + 1].bitcast(F32))

        def add_terms(engine, g, j, heads=slice(0, HEADS)):
            cols = slice(heads.start * D_ROPE, heads.stop * D_ROPE)
            engine.tensor_tensor(
                out=result[g][:, heads, j, D_NOPE:],
                in0=terms[g][:, j, 0, cols].rearrange("p (h d) -> p h d", d=D_ROPE),
                in1=terms[g][:, j, 1, cols].rearrange("p (h d) -> p h d", d=D_ROPE),
                op=ALU.add,
            )

        def store(g, heads=slice(0, HEADS)):
            b, w = divmod(g, GROUPS_PER_BATCH)
            nc.sync.dma_start(
                out=out_view[b, :, heads, TILES * w : TILES * (w + 1), :], in_=result[g][:, heads]
            )

        turns = consts.tile([P, 2, N_ANGLES, POS_PER_PART], F32)
        whole = consts.tile([P, 2, N_ANGLES, POS_PER_PART], F32)
        angles = [P, N_ANGLES, POS_PER_PART]

        def nearest_integer(part):
            nc.vector.tensor_scalar(
                out=whole[:, part],
                in0=turns[:, part],
                scalar1=ROUND_MAGIC,
                scalar2=ROUND_MAGIC,
                op0=ALU.add,
                op1=ALU.subtract,
            )

        def take_off_integer(part):
            nc.vector.tensor_tensor(out=turns[:, part], in0=turns[:, part], in1=whole[:, part], op=ALU.subtract)

        nc.vector.tensor_tensor(
            out=turns[:, 0],
            in0=turns_per_pos[:].unsqueeze(2).to_broadcast(angles),
            in1=pos[:].unsqueeze(1).to_broadcast(angles),
            op=ALU.mult,
        )
        nc.vector.tensor_scalar(out=turns[:, 1], in0=turns[:, 0], scalar1=0.25, scalar2=None, op0=ALU.add)
        nearest_integer(0)
        nearest_integer(1)
        take_off_integer(0)
        take_off_integer(1)

        warm_acc = psum_q.tile([P, P], F32, name="warm_acc", tag="q_rope")
        for repeat in range(16):
            nc.tensor.matmul(out=warm_acc[:], lhsT=ones[:], rhs=ones[:], start=True, stop=True)
        for j in range(TILES):
            transpose_x(0, tiles=slice(j, j + 1))
        waves = consts.tile([P, 2, N_ANGLES, POS_PER_PART], F32)
        nc.scalar.activation(out=waves[:], in_=turns[:], func=ACT.Sin, scale=2.0 * math.pi)
        nc.scalar.activation(out=warm[:], in_=eps[:], func=ACT.Abs_reciprocal_sqrt)
        rot = consts.tile([P, POS_PER_PART, 2, PAIRS, 2], F32)
        for e, o, part, sign in ((0, 0, 1, 1.0), (0, 1, 0, 1.0), (1, 0, 0, -1.0), (1, 1, 1, 1.0)):
            nc.gpsimd.tensor_scalar(
                out=rot[:, :, e, :, o],
                in0=waves[:, part].rearrange("p (i o) t -> p o t i", o=2)[:, o],
                scalar1=sign,
                scalar2=0.0,
                op0=ALU.mult,
                op1=ALU.add,
            )
        wqb_scales = consts.tile([P, 2 * HALF_COLS], U8, align_bytes=64)
        nc.gpsimd.tensor_copy(
            out=wqb_scales[:].bitcast(I32).rearrange("p (half h d) -> p half h d", half=2, d=D_NOPE // 4),
            in_=wqb_scale_rows[:].bitcast(I32).rearrange("p (h half d) -> p half h d", half=2, d=D_NOPE // 4),
        )
        gain_acc = psum_q.tile([P, RANK], F32, name="gain_acc", tag="q_nope")
        nc.tensor.matmul(out=gain_acc[:], lhsT=ones[:], rhs=gain_row[:], start=True, stop=True)
        for j in range(TILES):
            quantise(-1, j, j + 1)
        transpose_x(1, nc.vector.tensor_copy)
        gain = consts.tile([P, RANK], F32)
        nc.vector.tensor_copy(out=gain[:], in_=gain_acc[:])
        first_matmul(0, psum_front, "front", norm_by_tile=True)
        transpose_x(2)
        quantise_round(0)
        first_matmul(1, psum_q, "q_rope")
        inverse_norm(1)

        def live(g):
            return 0 <= g < N_GROUPS

        for i in range(1, N_GROUPS + 3):
            if live(i - 1):
                h = normalise(i - 1)
            if live(i) and i > 1:
                first_matmul(i, psum_front, "front")
                inverse_norm(i)
            if live(i - 1):
                transpose_h(i - 1, h)
            if live(i + 2):
                transpose_x(i + 2)
            if live(i + 1) or live(i - 2):
                quantise_round(i)
            if live(i - 4) and live(i - 3):
                if live(i + 1):
                    hold_gpsimd_for(i, X_PART)
                elif live(i - 2):
                    hold_gpsimd_for(i, H_PART)
                add_terms(nc.gpsimd, i - 4, TILES - 1)
                store(i - 4)
            for j in range(TILES):
                if live(i - 3) and live(i - 2):
                    rotate_terms(i - 3, j)
                    if j < TILES - 1:
                        add_terms(nc.gpsimd, i - 3, j)
                if live(i - 2):
                    second_matmul(i - 2, j)

        last = N_GROUPS - 1
        first_heads, last_heads = slice(0, HEADS // 2), slice(HEADS // 2, HEADS)
        rotate_terms(last, 0)
        rotate_terms(last, 1, first_heads)
        add_terms(nc.vector, last, 0)
        add_terms(nc.vector, last, 1, first_heads)
        store(last, first_heads)
        rotate_terms(last, 1, last_heads)
        add_terms(nc.vector, last, 1, last_heads)
        store(last, last_heads)
